import numpy as np
import ml_dtypes


def mxq(x, axis, fmt="e4m3"):
    dtype, down = {"e4m3": (ml_dtypes.float8_e4m3fn, 7), "e5m2": (ml_dtypes.float8_e5m2, 14)}[fmt]
    v = np.moveaxis(np.asarray(x, np.float32).astype(ml_dtypes.bfloat16).astype(np.float64), axis, -1)
    blocks = v.reshape(v.shape[:-1] + (-1, 32))
    amax = np.abs(blocks).max(-1, keepdims=True)
    byte = np.maximum(np.where(amax > 0, np.frexp(amax)[1] - 1 + 127, 0) - down, 1)
    scale = np.exp2(byte - 127.0)
    codes = (blocks / scale).astype(np.float32).astype(dtype).astype(np.float64)
    return np.moveaxis((codes * scale).reshape(v.shape), -1, axis)


WIDE = False


def mx_kscale(k):
    if not WIDE:
        return np.ones(k)
    levels = np.array([20, -20, 10, -10, 0])
    a = np.random.permutation(np.resize(levels, k // 512 * 4)).reshape(k // 512, 4)
    idx = np.arange(k)
    return np.exp2(a[idx // 512, idx % 128 // 32])


BF16 = ml_dtypes.bfloat16


def bf(x):
    return np.asarray(x, np.float32).astype(BF16)


def f64(x):
    return np.asarray(x).astype(np.float64)


B, IN, OUT, G, P = 8192, 64, 512, 5, 3
NB = G + P
K = IN * NB
LO, HI = -1.0, 1.0


def make_knots():
    gap = (HI - LO) / G
    return f64(np.arange(-P, G + P + 1)) * gap + LO


def b_splines(x, t, order):
    xg = x[:, :, None]
    bases = np.where((xg >= t[:-1]) & (xg < t[1:]), 1.0, 0.0)
    for k in range(1, order + 1):
        left = (xg - t[:-(k + 1)]) / (t[k:-1] - t[:-(k + 1)])
        right = (t[k + 1:] - xg) / (t[k + 1:] - t[1:-k])
        bases = left * bases[:, :, :-1] + right * bases[:, :, 1:]
    return bases


def d_b_splines(x, t):
    n2 = b_splines(x, t, P - 1)
    return P * (n2[:, :, :-1] / (t[P:-1] - t[:-(P + 1)]) - n2[:, :, 1:] / (t[P + 1:] - t[1:-P]))


def setup_inputs():
    u = mx_kscale(OUT)
    x = np.random.standard_normal((B, IN))
    w = np.random.standard_normal((OUT, IN, NB)) * 3.2 / np.sqrt(IN) / u[:, None, None]
    g = np.random.standard_normal((B, OUT)) * np.exp2(np.random.randint(-12, 1, (B, 1))) * u
    return {"x": bf(x), "spline_weight": bf(w), "grad_out": bf(g)}


def reference(x, spline_weight, grad_out):
    gq = mxq(f64(grad_out), 1, "e5m2")
    wq = mxq(f64(spline_weight).reshape(OUT, K), 0, "e4m3")
    m = gq @ wq
    d = d_b_splines(f64(x), make_knots())
    return (m.reshape(B, IN, NB) * d).sum(axis=2)

@@ -1,0 +1,168 @@
+from contextlib import ExitStack
+
+import concourse.bass as bass
+import concourse.mybir as mybir
+import concourse.tile as tile
+from concourse.masks import make_identity
+
+F32 = mybir.dt.float32
+BF16 = mybir.dt.bfloat16
+U32 = mybir.dt.uint32
+U8 = mybir.dt.uint8
+E4X4 = mybir.dt.float8_e4m3fn_x4
+E5X4 = mybir.dt.float8_e5m2_x4
+ALU = mybir.AluOpType
+ACT = mybir.ActivationFunctionType
+
+P = 128
+B, IN, OUT, NB = 8192, 64, 512, 8
+K = IN * NB
+NT = B // P
+CT = 8
+NCH = NT // CT
+ORDER = [3, 0, 1, 2, 7, 4, 5, 6]
+
+FLOPS = 2 * B * OUT * K
+
+
+def tile_kanlinearnores_t_kernel(tc, x, spline_weight, grad_out, out):
+    nc = tc.nc
+    g_v = grad_out.rearrange("(p t) k -> p t k", t=NT)
+    x_v = x.rearrange("(p t) i -> p t i", t=NT)
+    o_v = out.rearrange("(p t) i -> p t i", t=NT)
+    w2 = spline_weight.rearrange("o i g -> o (i g)")
+
+    with ExitStack() as ctx:
+        keep = ctx.enter_context(tc.tile_pool(name="keep", bufs=1))
+        gin = ctx.enter_context(tc.tile_pool(name="gin", bufs=3))
+        two = ctx.enter_context(tc.tile_pool(name="two", bufs=2))
+        psum_t = ctx.enter_context(tc.psum_pool(name="psum_t", bufs=3))
+        psum_m = ctx.enter_context(tc.psum_pool(name="psum_m", bufs=5))
+
+        w_raw = keep.tile([P, 4, K], BF16)
+        for u in range(2):
+            nc.scalar.dma_start(
+                out=w_raw[:, 2 * u : 2 * u + 2, :],
+                in_=w2[256 * u : 256 * u + 256, :].rearrange("(q e) c -> q e c", e=2),
+            )
+        x_sb = keep.tile([P, NT, IN], BF16)
+        nc.scalar.dma_start(out=x_sb[:], in_=x_v)
+
+        g_tiles = {}
+
+        def load(c):
+            g_sb = gin.tile([P, CT, OUT], BF16, name="g_sb")
+            nc.sync.dma_start(out=g_sb[:], in_=g_v[:, c * CT : (c + 1) * CT, :])
+            g_tiles[c] = g_sb
+
+        load(0)
+        load(1)
+
+        ident = keep.tile([P, P], F32)
+        make_identity(nc, ident[:])
+
+        w_grp = keep.tile([P, K, 4], BF16, align_bytes=64)
+        w_view = w_raw[:].rearrange("p t (i g) -> p g i t", g=NB)
+        for pos0, g0, n in ((0, 3, 1), (1, 0, 3), (4, 7, 1), (5, 4, 3)):
+            nc.vector.tensor_copy(
+                out=w_grp[:, pos0 * IN : (pos0 + n) * IN, :].rearrange("p (g i) t -> p g i t", g=n),
+                in_=w_view[:, g0 : g0 + n, :, :],
+            )
+        w_codes = keep.tile([P, K], U32, align_bytes=64)
+        w_scales = keep.tile([P, K], U8, align_bytes=64)
+        nc.vector.quantize_mx(
+            out=w_codes[:].bitcast(E4X4),
+            scales=w_scales[:],
+            in_=w_grp[:].rearrange("p c t -> p (c t)"),
+        )
+
+        xc = keep.tile([P, NT, IN], BF16)
+        nc.vector.tensor_scalar(out=xc[:], in0=x_sb[:], scalar1=-4.0, scalar2=4.0, op0=ALU.max, op1=ALU.min)
+
+        state = {}
+
+        def stage_a(c):
+            g32 = g_tiles[c][:].bitcast(F32)
+            grp = two.tile([P, CT * P, 2], F32, name="grp", align_bytes=64)
+            for h in range(CT // 2):
+                pt = psum_t.tile([P, 2, 2, P], F32, name="pt")
+                for j in range(2):
+                    for u in range(2):
+                        nc.tensor.transpose(pt[:, j, u, :], g32[:, 2 * h + j, P * u : P * u + P], ident[:])
+                nc.scalar.copy(
+                    out=grp[:, 2 * h * P : (2 * h + 2) * P, :].rearrange("p (j r) u -> p j r u", j=2),
+                    in_=pt[:].rearrange("p j u r -> p j r u"),
+                )
+            g_codes = two.tile([P, CT * P], U32, name="g_codes", align_bytes=64)
+            g_scales = two.tile([P, CT * P], U8, name="g_scales", align_bytes=64)
+            nc.vector.quantize_mx(
+                out=g_codes[:].bitcast(E5X4),
+                scales=g_scales[:],
+                in_=grp[:].rearrange("p r u -> p (r u)").bitcast(BF16),
+            )
+            ab = two.tile([P, CT, NB, IN], F32, name="ab")
+            xs = xc[:, c * CT : (c + 1) * CT, :]
+            for pos in range(NB):
+                nc.scalar.activation(out=ab[:, :, pos, :], in_=xs, func=ACT.Abs, bias=3.5 - ORDER[pos], scale=2.5)
+            bw = two.tile([P, CT, 2, IN], F32, name="bw")
+            nc.scalar.activation(out=bw[:], in_=ab[:, :, 0:6:5, :], func=ACT.Abs, bias=-2.0, scale=1.0)
+            nc.scalar.activation(out=bw[:], in_=bw[:], func=ACT.Abs, bias=-2.0, scale=1.0)
+            w = two.tile([P, CT, 2, IN], F32, name="w")
+            nc.gpsimd.tensor_scalar(out=w[:], in0=bw[:], scalar1=-1.0, scalar2=1.0, op0=ALU.add, op1=ALU.mult)
+            ws = two.tile([P, CT, 2, IN], F32, name="ws")
+            for j in range(2):
+                nc.gpsimd.tensor_scalar(
+                    out=ws[:, :, j, :], in0=bw[:, :, 1 - j, :], scalar1=-1.0, scalar2=1.25, op0=ALU.add, op1=ALU.mult
+                )
+            mn = two.tile([P, CT, 2 * IN], F32, name="mn")
+            mx = two.tile([P, CT, 2 * IN], F32, name="mx")
+            wf = w[:].rearrange("p c j i -> p c (j i)")
+            nc.vector.scalar_tensor_tensor(out=mn[:], in0=wf, scalar=3.0, in1=wf, op0=ALU.mult, op1=ALU.min)
+            nc.vector.scalar_tensor_tensor(out=mx[:], in0=wf, scalar=3.0, in1=wf, op0=ALU.mult, op1=ALU.max)
+            state[c] = (g_codes, g_scales, ab, ws, mn, mx)
+
+        def stage_b(c):
+            g_codes, g_scales, ab, ws, mn, mx = state[c]
+            tm = two.tile([P, CT, K], F32, name="tm")
+            for j in range(CT):
+                pm = psum_m.tile([P, K], F32, name="pm")
+                nc.tensor.matmul_mx(
+                    out=pm[:],
+                    lhsT=g_codes[:, j * P : (j + 1) * P].bitcast(E5X4),
+                    lhsT_scale=g_scales[:, j * P : (j + 1) * P],
+                    rhs=w_codes[:].bitcast(E4X4),
+                    rhs_scale=w_scales[:],
+                    start=True,
+                    stop=True,
+                )
+                nc.vector.scalar_tensor_tensor(
+                    out=tm[:, j, :],
+                    in0=ab[:, j, :, :].rearrange("p g i -> p (g i)"),
+                    scalar=2.0,
+                    in1=pm[:],
+                    op0=ALU.is_lt,
+                    op1=ALU.mult,
+                )
+            s = two.tile([P, CT, K // 2], F32, name="s")
+            nc.gpsimd.tensor_tensor(out=s[:], in0=tm[:, :, 0 : K // 2], in1=tm[:, :, K // 2 : K], op=ALU.add)
+            e1 = two.tile([P, CT, 2 * IN], F32, name="e1")
+            e2 = two.tile([P, CT, 2 * IN], F32, name="e2")
+            nc.vector.scalar_tensor_tensor(
+                out=e1[:], in0=mn[:], scalar=-1.0, in1=s[:, :, 0 : 2 * IN], op0=ALU.add, op1=ALU.mult
+            )
+            nc.vector.scalar_tensor_tensor(
+                out=e2[:], in0=mx[:], scalar=1.0, in1=s[:, :, 2 * IN : 4 * IN], op0=ALU.add, op1=ALU.mult
+            )
+            nc.gpsimd.tensor_tensor(out=e1[:], in0=e1[:], in1=e2[:], op=ALU.add)
+            nc.vector.tensor_tensor(out=e2[:], in0=e1[:], in1=ws[:].rearrange("p c j i -> p c (j i)"), op=ALU.mult)
+            o = two.tile([P, CT, IN], F32, name="o")
+            nc.gpsimd.tensor_tensor(out=o[:], in0=e2[:, :, IN : 2 * IN], in1=e2[:, :, 0:IN], op=ALU.subtract)
+            nc.sync.dma_start(out=o_v[:, c * CT : (c + 1) * CT, :], in_=o[:])
+
+        stage_a(0)
+        for c in range(NCH):
+            if c + 2 < NCH:
+                load(c + 2)
+            if c + 1 < NCH:
+                stage_a(c + 1)
+            stage_b(c)

@@ -1,8 +1,6 @@
 from contextlib import ExitStack
 
-import concourse.bass as bass
 import concourse.mybir as mybir
-import concourse.tile as tile
 from concourse.masks import make_identity
 
 F32 = mybir.dt.float32
@@ -21,6 +19,7 @@ NT = B // P
 CT = 8
 NCH = NT // CT
 ORDER = [3, 0, 1, 2, 7, 4, 5, 6]
+WAVE_PLANES = (0, 5)
 
 FLOPS = 2 * B * OUT * K
 
@@ -33,11 +32,12 @@ def tile_kanlinearnores_t_kernel(tc, x, spline_weight, grad_out, out):
     w2 = spline_weight.rearrange("o i g -> o (i g)")
 
     with ExitStack() as ctx:
+        ctx.enter_context(tc.manual_schedule())
         keep = ctx.enter_context(tc.tile_pool(name="keep", bufs=1))
-        gin = ctx.enter_context(tc.tile_pool(name="gin", bufs=3))
         two = ctx.enter_context(tc.tile_pool(name="two", bufs=2))
-        psum_t = ctx.enter_context(tc.psum_pool(name="psum_t", bufs=3))
-        psum_m = ctx.enter_context(tc.psum_pool(name="psum_m", bufs=5))
+        three = ctx.enter_context(tc.tile_pool(name="three", bufs=3))
+        psum_t = ctx.enter_context(tc.psum_pool(name="psum_t", bufs=4))
+        psum_m = ctx.enter_context(tc.psum_pool(name="psum_m", bufs=4))
 
         w_raw = keep.tile([P, 4, K], BF16)
         for u in range(2):
@@ -45,18 +45,22 @@ def tile_kanlinearnores_t_kernel(tc, x, spline_weight, grad_out, out):
                 out=w_raw[:, 2 * u : 2 * u + 2, :],
                 in_=w2[256 * u : 256 * u + 256, :].rearrange("(q e) c -> q e c", e=2),
             )
-        x_sb = keep.tile([P, NT, IN], BF16)
-        nc.scalar.dma_start(out=x_sb[:], in_=x_v)
+        xc = keep.tile([P, NT, IN], BF16)
+        nc.scalar.dma_start(out=xc[:], in_=x_v)
 
-        g_tiles = {}
+        st = {}
+
+        def live(c):
+            return 0 <= c < NCH
 
         def load(c):
-            g_sb = gin.tile([P, CT, OUT], BF16, name="g_sb")
+            g_sb = three.tile([P, CT, OUT], BF16, name="g_sb")
             nc.sync.dma_start(out=g_sb[:], in_=g_v[:, c * CT : (c + 1) * CT, :])
-            g_tiles[c] = g_sb
+            st["g", c] = g_sb
 
         load(0)
         load(1)
+        load(2)
 
         ident = keep.tile([P, P], F32)
         make_identity(nc, ident[:])
@@ -70,60 +74,82 @@ def tile_kanlinearnores_t_kernel(tc, x, spline_weight, grad_out, out):
             )
         w_codes = keep.tile([P, K], U32, align_bytes=64)
         w_scales = keep.tile([P, K], U8, align_bytes=64)
+        nc.vector.tensor_scalar(out=xc[:], in0=xc[:], scalar1=-4.0, scalar2=4.0, op0=ALU.max, op1=ALU.min)
         nc.vector.quantize_mx(
             out=w_codes[:].bitcast(E4X4),
             scales=w_scales[:],
             in_=w_grp[:].rearrange("p c t -> p (c t)"),
         )
 
-        xc = keep.tile([P, NT, IN], BF16)
-        nc.vector.tensor_scalar(out=xc[:], in0=x_sb[:], scalar1=-4.0, scalar2=4.0, op0=ALU.max, op1=ALU.min)
-
-        state = {}
-
-        def stage_a(c):
-            g32 = g_tiles[c][:].bitcast(F32)
+        def transposes(c):
+            g32 = st["g", c][:].bitcast(F32)
             grp = two.tile([P, CT * P, 2], F32, name="grp", align_bytes=64)
+            st["grp", c] = grp
+            pts = []
             for h in range(CT // 2):
                 pt = psum_t.tile([P, 2, 2, P], F32, name="pt")
                 for j in range(2):
                     for u in range(2):
                         nc.tensor.transpose(pt[:, j, u, :], g32[:, 2 * h + j, P * u : P * u + P], ident[:])
+                pts.append(pt)
+            for h in range(CT // 2):
                 nc.scalar.copy(
                     out=grp[:, 2 * h * P : (2 * h + 2) * P, :].rearrange("p (j r) u -> p j r u", j=2),
-                    in_=pt[:].rearrange("p j u r -> p j r u"),
+                    in_=pts[h][:].rearrange("p j u r -> p j r u"),
                 )
+
+        def quantise(c):
             g_codes = two.tile([P, CT * P], U32, name="g_codes", align_bytes=64)
             g_scales = two.tile([P, CT * P], U8, name="g_scales", align_bytes=64)
             nc.vector.quantize_mx(
                 out=g_codes[:].bitcast(E5X4),
                 scales=g_scales[:],
-                in_=grp[:].rearrange("p r u -> p (r u)").bitcast(BF16),
+                in_=st["grp", c][:].rearrange("p r u -> p (r u)").bitcast(BF16),
             )
+            st["codes", c] = (g_codes, g_scales)
+
+        def ab_plane(c, pos):
+            nc.scalar.activation(
+                out=st["ab", c][:, :, pos, :],
+                in_=xc[:, c * CT : (c + 1) * CT, :],
+                func=ACT.Abs,
+                bias=3.5 - ORDER[pos],
+                scale=2.5,
+            )
+
+        def waves(c):
             ab = two.tile([P, CT, NB, IN], F32, name="ab")
-            xs = xc[:, c * CT : (c + 1) * CT, :]
-            for pos in range(NB):
-                nc.scalar.activation(out=ab[:, :, pos, :], in_=xs, func=ACT.Abs, bias=3.5 - ORDER[pos], scale=2.5)
-            bw = two.tile([P, CT, 2, IN], F32, name="bw")
+            st["ab", c] = ab
+            for pos in WAVE_PLANES:
+                ab_plane(c, pos)
+            bw = three.tile([P, CT, 2, IN], F32, name="bw")
             nc.scalar.activation(out=bw[:], in_=ab[:, :, 0:6:5, :], func=ACT.Abs, bias=-2.0, scale=1.0)
             nc.scalar.activation(out=bw[:], in_=bw[:], func=ACT.Abs, bias=-2.0, scale=1.0)
-            w = two.tile([P, CT, 2, IN], F32, name="w")
-            nc.gpsimd.tensor_scalar(out=w[:], in0=bw[:], scalar1=-1.0, scalar2=1.0, op0=ALU.add, op1=ALU.mult)
-            ws = two.tile([P, CT, 2, IN], F32, name="ws")
-            for j in range(2):
-                nc.gpsimd.tensor_scalar(
-                    out=ws[:, :, j, :], in0=bw[:, :, 1 - j, :], scalar1=-1.0, scalar2=1.25, op0=ALU.add, op1=ALU.mult
-                )
-            mn = two.tile([P, CT, 2 * IN], F32, name="mn")
-            mx = two.tile([P, CT, 2 * IN], F32, name="mx")
-            wf = w[:].rearrange("p c j i -> p c (j i)")
-            nc.vector.scalar_tensor_tensor(out=mn[:], in0=wf, scalar=3.0, in1=wf, op0=ALU.mult, op1=ALU.min)
-            nc.vector.scalar_tensor_tensor(out=mx[:], in0=wf, scalar=3.0, in1=wf, op0=ALU.mult, op1=ALU.max)
-            state[c] = (g_codes, g_scales, ab, ws, mn, mx)
+            w = two.tile([P, CT, 2 * IN], F32, name="w")
+            nc.scalar.activation(
+                out=w[:], in_=bw[:].rearrange("p c j i -> p c (j i)"), func=ACT.Identity, bias=-1.25, scale=1.25
+            )
+            st["bw", c] = bw
+            st["w", c] = w
 
-        def stage_b(c):
-            g_codes, g_scales, ab, ws, mn, mx = state[c]
+        def rest_of_ab(c):
+            for pos in range(NB):
+                if pos not in WAVE_PLANES:
+                    ab_plane(c, pos)
+
+        def slopes(c, which):
+            w = st["w", c]
+            t = three.tile([P, CT, 2 * IN], F32, name=which)
+            nc.vector.scalar_tensor_tensor(
+                out=t[:], in0=w[:], scalar=3.0, in1=w[:], op0=ALU.mult, op1=(ALU.min if which == "mn" else ALU.max)
+            )
+            st[which, c] = t
+
+        def products(c):
+            g_codes, g_scales = st["codes", c]
+            ab = st["ab", c]
             tm = two.tile([P, CT, K], F32, name="tm")
+            st["tm", c] = tm
             for j in range(CT):
                 pm = psum_m.tile([P, K], F32, name="pm")
                 nc.tensor.matmul_mx(
@@ -143,26 +169,59 @@ def tile_kanlinearnores_t_kernel(tc, x, spline_weight, grad_out, out):
                     op0=ALU.is_lt,
                     op1=ALU.mult,
                 )
+
+        def fold(c):
+            tm = st["tm", c]
             s = two.tile([P, CT, K // 2], F32, name="s")
             nc.gpsimd.tensor_tensor(out=s[:], in0=tm[:, :, 0 : K // 2], in1=tm[:, :, K // 2 : K], op=ALU.add)
-            e1 = two.tile([P, CT, 2 * IN], F32, name="e1")
-            e2 = two.tile([P, CT, 2 * IN], F32, name="e2")
-            nc.vector.scalar_tensor_tensor(
-                out=e1[:], in0=mn[:], scalar=-1.0, in1=s[:, :, 0 : 2 * IN], op0=ALU.add, op1=ALU.mult
-            )
-            nc.vector.scalar_tensor_tensor(
-                out=e2[:], in0=mx[:], scalar=1.0, in1=s[:, :, 2 * IN : 4 * IN], op0=ALU.add, op1=ALU.mult
-            )
-            nc.gpsimd.tensor_tensor(out=e1[:], in0=e1[:], in1=e2[:], op=ALU.add)
-            nc.vector.tensor_tensor(out=e2[:], in0=e1[:], in1=ws[:].rearrange("p c j i -> p c (j i)"), op=ALU.mult)
-            o = two.tile([P, CT, IN], F32, name="o")
-            nc.gpsimd.tensor_tensor(out=o[:], in0=e2[:, :, IN : 2 * IN], in1=e2[:, :, 0:IN], op=ALU.subtract)
-            nc.sync.dma_start(out=o_v[:, c * CT : (c + 1) * CT, :], in_=o[:])
+            st["s", c] = s
 
-        stage_a(0)
-        for c in range(NCH):
-            if c + 2 < NCH:
-                load(c + 2)
-            if c + 1 < NCH:
-                stage_a(c + 1)
-            stage_b(c)
+        for k in range(-2, NCH + 1):
+            if live(k + 3) and k + 3 > 2:
+                load(k + 3)
+            if live(k - 1):
+                fold(k - 1)
+            if live(k):
+                products(k)
+            if live(k + 1):
+                waves(k + 1)
+            d = k - 1
+            if live(d):
+                s = st["s", d]
+                bw = st["bw", d]
+                e1 = two.tile([P, CT, 2, IN], F32, name="e1")
+                e2 = two.tile([P, CT, 2, IN], F32, name="e2")
+                e1f = e1[:].rearrange("p c j i -> p c (j i)")
+                e2f = e2[:].rearrange("p c j i -> p c (j i)")
+                nc.vector.scalar_tensor_tensor(
+                    out=e1f, in0=st["mn", d][:], scalar=-1.25, in1=s[:, :, 0 : 2 * IN], op0=ALU.add, op1=ALU.mult
+                )
+                nc.vector.scalar_tensor_tensor(
+                    out=e2f, in0=st["mx", d][:], scalar=1.25, in1=s[:, :, 2 * IN : 4 * IN], op0=ALU.add, op1=ALU.mult
+                )
+            if live(k + 1):
+                quantise(k + 1)
+            if live(d):
+                nc.vector.tensor_tensor(out=e1f, in0=e1f, in1=e2f, op=ALU.add)
+            if live(k + 1):
+                slopes(k + 1, "mn")
+            if live(d):
+                for j in range(2):
+                    nc.vector.scalar_tensor_tensor(
+                        out=e2[:, :, j, :],
+                        in0=bw[:, :, 1 - j, :],
+                        scalar=-1.0,
+                        in1=e1[:, :, j, :],
+                        op0=ALU.add,
+                        op1=ALU.mult,
+                    )
+            if live(k + 1):
+                slopes(k + 1, "mx")
+            if live(d):
+                o = two.tile([P, CT, IN], F32, name="o")
+                nc.vector.tensor_tensor(out=o[:], in0=e2[:, :, 1, :], in1=e2[:, :, 0, :], op=ALU.subtract)
+                nc.sync.dma_start(out=o_v[:, d * CT : (d + 1) * CT, :], in_=o[:])
+            if live(k + 1):
+                rest_of_ab(k + 1)
+            if live(k + 2):
+                transposes(k + 2)

@@ -16,10 +16,13 @@ P = 128
 B, IN, OUT, NB = 8192, 64, 512, 8
 K = IN * NB
 NT = B // P
-CT = 8
-NCH = NT // CT
-ORDER = [3, 0, 1, 2, 7, 4, 5, 6]
-WAVE_PLANES = (0, 5)
+SIZES = [4,4,4,4,4,4,4,4,4,4,4,4,4,4,4,4]
+NCH = len(SIZES)
+STARTS = [sum(SIZES[:c]) for c in range(NCH)]
+X_HEAD = 8
+ORDER = [0, 3, 2, 1, 4, 7, 6, 5]
+WAVE_PLANES = (1, 4)
+G_BUFS = 4
 
 FLOPS = 2 * B * OUT * K
 
@@ -36,71 +39,87 @@ def tile_kanlinearnores_t_kernel(tc, x, spline_weight, grad_out, out):
         keep = ctx.enter_context(tc.tile_pool(name="keep", bufs=1))
         two = ctx.enter_context(tc.tile_pool(name="two", bufs=2))
         three = ctx.enter_context(tc.tile_pool(name="three", bufs=3))
+        gin = ctx.enter_context(tc.tile_pool(name="gin", bufs=G_BUFS))
         psum_t = ctx.enter_context(tc.psum_pool(name="psum_t", bufs=4))
-        psum_m = ctx.enter_context(tc.psum_pool(name="psum_m", bufs=4))
-
-        w_raw = keep.tile([P, 4, K], BF16)
-        for u in range(2):
-            nc.scalar.dma_start(
-                out=w_raw[:, 2 * u : 2 * u + 2, :],
-                in_=w2[256 * u : 256 * u + 256, :].rearrange("(q e) c -> q e c", e=2),
-            )
-        xc = keep.tile([P, NT, IN], BF16)
-        nc.scalar.dma_start(out=xc[:], in_=x_v)
+        psum_m = ctx.enter_context(tc.psum_pool(name="psum_m", bufs=3))
+        psum_o = ctx.enter_context(tc.psum_pool(name="psum_o", bufs=1))
 
         st = {}
 
         def live(c):
             return 0 <= c < NCH
 
+        def span(c):
+            return slice(STARTS[c], STARTS[c] + SIZES[c])
+
         def load(c):
-            g_sb = three.tile([P, CT, OUT], BF16, name="g_sb")
-            nc.sync.dma_start(out=g_sb[:], in_=g_v[:, c * CT : (c + 1) * CT, :])
+            g_sb = gin.tile([P, SIZES[c], OUT], BF16, name="g_sb")
+            nc.sync.dma_start(out=g_sb[:], in_=g_v[:, span(c), :])
             st["g", c] = g_sb
 
+        w_raw = keep.tile([P, 4, K], BF16)
+        for u in range(2):
+            nc.sync.dma_start(
+                out=w_raw[:, 2 * u : 2 * u + 2, :],
+                in_=w2[256 * u : 256 * u + 256, :].rearrange("(q e) c -> q e c", e=2),
+            )
+        xc = keep.tile([P, NT, IN], BF16)
+        nc.sync.dma_start(out=xc[:, 0:X_HEAD, :], in_=x_v[:, 0:X_HEAD, :])
         load(0)
         load(1)
-        load(2)
+        nc.sync.dma_start(out=xc[:, X_HEAD:NT, :], in_=x_v[:, X_HEAD:NT, :])
+        for c in range(2, G_BUFS):
+            load(c)
 
         ident = keep.tile([P, P], F32)
         make_identity(nc, ident[:])
+        ident_neg = keep.tile([P, P], F32)
+        nc.gpsimd.tensor_scalar(out=ident_neg[:], in0=ident[:], scalar1=-1.0, scalar2=0.0, op0=ALU.mult, op1=ALU.add)
 
+        nc.vector.tensor_scalar(
+            out=xc[:, 0:X_HEAD, :], in0=xc[:, 0:X_HEAD, :], scalar1=-4.0, scalar2=4.0, op0=ALU.max, op1=ALU.min
+        )
         w_grp = keep.tile([P, K, 4], BF16, align_bytes=64)
         w_view = w_raw[:].rearrange("p t (i g) -> p g i t", g=NB)
-        for pos0, g0, n in ((0, 3, 1), (1, 0, 3), (4, 7, 1), (5, 4, 3)):
-            nc.vector.tensor_copy(
-                out=w_grp[:, pos0 * IN : (pos0 + n) * IN, :].rearrange("p (g i) t -> p g i t", g=n),
-                in_=w_view[:, g0 : g0 + n, :, :],
-            )
+        for pos in range(NB):
+            nc.vector.tensor_copy(out=w_grp[:, pos * IN : (pos + 1) * IN, :], in_=w_view[:, ORDER[pos], :, :])
         w_codes = keep.tile([P, K], U32, align_bytes=64)
         w_scales = keep.tile([P, K], U8, align_bytes=64)
-        nc.vector.tensor_scalar(out=xc[:], in0=xc[:], scalar1=-4.0, scalar2=4.0, op0=ALU.max, op1=ALU.min)
         nc.vector.quantize_mx(
             out=w_codes[:].bitcast(E4X4),
             scales=w_scales[:],
             in_=w_grp[:].rearrange("p c t -> p (c t)"),
         )
+        nc.vector.tensor_scalar(
+            out=xc[:, X_HEAD:NT, :], in0=xc[:, X_HEAD:NT, :], scalar1=-4.0, scalar2=4.0, op0=ALU.max, op1=ALU.min
+        )
 
         def transposes(c):
+            n = SIZES[c]
             g32 = st["g", c][:].bitcast(F32)
-            grp = two.tile([P, CT * P, 2], F32, name="grp", align_bytes=64)
-            st["grp", c] = grp
             pts = []
-            for h in range(CT // 2):
+            for h in range(n // 2):
                 pt = psum_t.tile([P, 2, 2, P], F32, name="pt")
                 for j in range(2):
                     for u in range(2):
                         nc.tensor.transpose(pt[:, j, u, :], g32[:, 2 * h + j, P * u : P * u + P], ident[:])
                 pts.append(pt)
-            for h in range(CT // 2):
+            st["pts", c] = pts
+
+        def regroup(c):
+            n = SIZES[c]
+            grp = two.tile([P, n * P, 2], F32, name="grp", align_bytes=64)
+            st["grp", c] = grp
+            for h in range(n // 2):
                 nc.scalar.copy(
                     out=grp[:, 2 * h * P : (2 * h + 2) * P, :].rearrange("p (j r) u -> p j r u", j=2),
-                    in_=pts[h][:].rearrange("p j u r -> p j r u"),
+                    in_=st["pts", c][h][:].rearrange("p j u r -> p j r u"),
                 )
 
         def quantise(c):
-            g_codes = two.tile([P, CT * P], U32, name="g_codes", align_bytes=64)
-            g_scales = two.tile([P, CT * P], U8, name="g_scales", align_bytes=64)
+            n = SIZES[c]
+            g_codes = two.tile([P, n * P], U32, name="g_codes", align_bytes=64)
+            g_scales = two.tile([P, n * P], U8, name="g_scales", align_bytes=64)
             nc.vector.quantize_mx(
                 out=g_codes[:].bitcast(E5X4),
                 scales=g_scales[:],
@@ -108,49 +127,34 @@ def tile_kanlinearnores_t_kernel(tc, x, spline_weight, grad_out, out):
             )
             st["codes", c] = (g_codes, g_scales)
 
-        def ab_plane(c, pos):
-            nc.scalar.activation(
-                out=st["ab", c][:, :, pos, :],
-                in_=xc[:, c * CT : (c + 1) * CT, :],
-                func=ACT.Abs,
-                bias=3.5 - ORDER[pos],
-                scale=2.5,
-            )
+        def distances(c):
+            ab = two.tile([P, SIZES[c], NB, IN], F32, name="ab")
+            st["ab", c] = ab
+            for pos in range(NB):
+                nc.scalar.activation(
+                    out=ab[:, :, pos, :], in_=xc[:, span(c), :], func=ACT.Abs, bias=3.5 - ORDER[pos], scale=2.5
+                )
 
         def waves(c):
-            ab = two.tile([P, CT, NB, IN], F32, name="ab")
-            st["ab", c] = ab
-            for pos in WAVE_PLANES:
-                ab_plane(c, pos)
-            bw = three.tile([P, CT, 2, IN], F32, name="bw")
-            nc.scalar.activation(out=bw[:], in_=ab[:, :, 0:6:5, :], func=ACT.Abs, bias=-2.0, scale=1.0)
-            nc.scalar.activation(out=bw[:], in_=bw[:], func=ACT.Abs, bias=-2.0, scale=1.0)
-            w = two.tile([P, CT, 2 * IN], F32, name="w")
+            n = SIZES[c]
+            ab = st["ab", c]
+            bw = two.tile([P, 2, n, IN], F32, name="bw")
             nc.scalar.activation(
-                out=w[:], in_=bw[:].rearrange("p c j i -> p c (j i)"), func=ACT.Identity, bias=-1.25, scale=1.25
+                out=bw[:], in_=ab[:, :, 1:5:3, :].rearrange("p c j i -> p j c i"), func=ACT.Abs, bias=-2.0, scale=1.0
             )
-            st["bw", c] = bw
-            st["w", c] = w
-
-        def rest_of_ab(c):
-            for pos in range(NB):
-                if pos not in WAVE_PLANES:
-                    ab_plane(c, pos)
-
-        def slopes(c, which):
-            w = st["w", c]
-            t = three.tile([P, CT, 2 * IN], F32, name=which)
-            nc.vector.scalar_tensor_tensor(
-                out=t[:], in0=w[:], scalar=3.0, in1=w[:], op0=ALU.mult, op1=(ALU.min if which == "mn" else ALU.max)
-            )
-            st[which, c] = t
+            nc.scalar.activation(out=bw[:], in_=bw[:], func=ACT.Abs, bias=-2.0, scale=1.0)
+            w = two.tile([P, 2, n, IN], F32, name="w")
+            aw = two.tile([P, 2, n, IN], F32, name="aw")
+            nc.scalar.activation(out=w[:], in_=bw[:], func=ACT.Identity, bias=-1.25, scale=1.25)
+            nc.scalar.activation(out=aw[:], in_=bw[:], func=ACT.Abs, bias=-1.0, scale=1.0)
+            st["w", c] = (w, aw)
 
         def products(c):
             g_codes, g_scales = st["codes", c]
             ab = st["ab", c]
-            tm = two.tile([P, CT, K], F32, name="tm")
+            tm = two.tile([P, SIZES[c], K], F32, name="tm")
             st["tm", c] = tm
-            for j in range(CT):
+            for j in range(SIZES[c]):
                 pm = psum_m.tile([P, K], F32, name="pm")
                 nc.tensor.matmul_mx(
                     out=pm[:],
@@ -172,56 +176,71 @@ def tile_kanlinearnores_t_kernel(tc, x, spline_weight, grad_out, out):
 
         def fold(c):
             tm = st["tm", c]
-            s = two.tile([P, CT, K // 2], F32, name="s")
+            s = two.tile([P, SIZES[c], K // 2], F32, name="s")
             nc.gpsimd.tensor_tensor(out=s[:], in0=tm[:, :, 0 : K // 2], in1=tm[:, :, K // 2 : K], op=ALU.add)
             st["s", c] = s
 
-        for k in range(-2, NCH + 1):
-            if live(k + 3) and k + 3 > 2:
-                load(k + 3)
-            if live(k - 1):
-                fold(k - 1)
-            if live(k):
-                products(k)
-            if live(k + 1):
-                waves(k + 1)
+        def total(c):
+            u, t = st["ut", c]
+            po = psum_o.tile([P, SIZES[c] * IN], F32, name="po")
+            nc.tensor.matmul(out=po[:], lhsT=ident[:], rhs=u[:].rearrange("p c i -> p (c i)"), start=True, stop=False)
+            nc.tensor.matmul(
+                out=po[:], lhsT=ident[:], rhs=t[:, 0, :, :].rearrange("p c i -> p (c i)"), start=False, stop=False
+            )
+            nc.tensor.matmul(
+                out=po[:], lhsT=ident_neg[:], rhs=t[:, 1, :, :].rearrange("p c i -> p (c i)"), start=False, stop=True
+            )
+            st["po", c] = po
+
+        def store(c):
+            o = two.tile([P, SIZES[c] * IN], F32, name="o")
+            nc.scalar.copy(out=o[:], in_=st["po", c][:])
+            nc.sync.dma_start(out=o_v[:, span(c), :], in_=o[:].rearrange("p (c i) -> p c i", i=IN))
+
+        distances(0)
+        for k in range(-2, NCH + 2):
+            if live(k + G_BUFS - 1) and k + G_BUFS - 1 >= G_BUFS:
+                load(k + G_BUFS - 1)
             d = k - 1
             if live(d):
+                fold(d)
+            if live(k):
+                products(k)
+            if live(k + 2):
+                transposes(k + 2)
+            if live(k - 2):
+                total(k - 2)
+            if live(k + 1) and k + 1 > 0:
+                distances(k + 1)
+            if live(k):
+                waves(k)
+            if live(k + 2):
+                regroup(k + 2)
+            if live(k - 2):
+                store(k - 2)
+            if live(d):
+                n = SIZES[d]
+                w, aw = st["w", d]
                 s = st["s", d]
-                bw = st["bw", d]
-                e1 = two.tile([P, CT, 2, IN], F32, name="e1")
-                e2 = two.tile([P, CT, 2, IN], F32, name="e2")
-                e1f = e1[:].rearrange("p c j i -> p c (j i)")
-                e2f = e2[:].rearrange("p c j i -> p c (j i)")
+                first = s[:, :, 0 : 2 * IN].rearrange("p c (j i) -> p j c i", j=2)
+                second = s[:, :, 2 * IN : 4 * IN].rearrange("p c (j i) -> p j c i", j=2)
+                pi = keep.tile([P, n, IN], F32, name="pi")
+                ng = keep.tile([P, 2, n, IN], F32, name="ng")
+                sg = keep.tile([P, 2, n, IN], F32, name="sg")
+                dl = keep.tile([P, 2, n, IN], F32, name="dl")
+                ss = keep.tile([P, n, IN], F32, name="ss")
+                u = three.tile([P, n, IN], F32, name="u")
+                t = three.tile([P, 2, n, IN], F32, name="t")
+                st["ut", d] = (u, t)
+                nc.vector.scalar_tensor_tensor(out=ng[:], in0=aw[:], scalar=-2.0, in1=w[:], op0=ALU.add, op1=ALU.mult)
+                nc.vector.tensor_tensor(out=dl[:], in0=first, in1=second, op=ALU.subtract)
+                nc.vector.tensor_tensor(out=sg[:], in0=first, in1=second, op=ALU.add)
                 nc.vector.scalar_tensor_tensor(
-                    out=e1f, in0=st["mn", d][:], scalar=-1.25, in1=s[:, :, 0 : 2 * IN], op0=ALU.add, op1=ALU.mult
+                    out=pi[:], in0=w[:, 0, :, :], scalar=1.6, in1=w[:, 1, :, :], op0=ALU.mult, op1=ALU.mult
                 )
-                nc.vector.scalar_tensor_tensor(
-                    out=e2f, in0=st["mx", d][:], scalar=1.25, in1=s[:, :, 2 * IN : 4 * IN], op0=ALU.add, op1=ALU.mult
-                )
+                nc.vector.tensor_tensor(out=t[:], in0=dl[:], in1=ng[:], op=ALU.mult)
+                nc.vector.tensor_tensor(out=ss[:], in0=sg[:, 0, :, :], in1=sg[:, 1, :, :], op=ALU.subtract)
             if live(k + 1):
                 quantise(k + 1)
             if live(d):
-                nc.vector.tensor_tensor(out=e1f, in0=e1f, in1=e2f, op=ALU.add)
-            if live(k + 1):
-                slopes(k + 1, "mn")
-            if live(d):
-                for j in range(2):
-                    nc.vector.scalar_tensor_tensor(
-                        out=e2[:, :, j, :],
-                        in0=bw[:, :, 1 - j, :],
-                        scalar=-1.0,
-                        in1=e1[:, :, j, :],
-                        op0=ALU.add,
-                        op1=ALU.mult,
-                    )
-            if live(k + 1):
-                slopes(k + 1, "mx")
-            if live(d):
-                o = two.tile([P, CT, IN], F32, name="o")
-                nc.vector.tensor_tensor(out=o[:], in0=e2[:, :, 1, :], in1=e2[:, :, 0, :], op=ALU.subtract)
-                nc.sync.dma_start(out=o_v[:, d * CT : (d + 1) * CT, :], in_=o[:])
-            if live(k + 1):
-                rest_of_ab(k + 1)
-            if live(k + 2):
-                transposes(k + 2)
+                nc.vector.tensor_tensor(out=u[:], in0=ss[:], in1=pi[:], op=ALU.mult)

@@ -16,12 +16,13 @@ P = 128
 B, IN, OUT, NB = 8192, 64, 512, 8
 K = IN * NB
 NT = B // P
-SIZES = [4,4,4,4,4,4,4,4,4,4,4,4,4,4,4,4]
+SIZES = [4,4,4,4,4,4,4,4,4,4,4,4,4,4,4,2,2]
 NCH = len(SIZES)
 STARTS = [sum(SIZES[:c]) for c in range(NCH)]
 X_HEAD = 8
 ORDER = [0, 3, 2, 1, 4, 7, 6, 5]
 WAVE_PLANES = (1, 4)
+AHEAD = 3
 G_BUFS = 4
 
 FLOPS = 2 * B * OUT * K
@@ -73,8 +74,6 @@ def tile_kanlinearnores_t_kernel(tc, x, spline_weight, grad_out, out):
 
         ident = keep.tile([P, P], F32)
         make_identity(nc, ident[:])
-        ident_neg = keep.tile([P, P], F32)
-        nc.gpsimd.tensor_scalar(out=ident_neg[:], in0=ident[:], scalar1=-1.0, scalar2=0.0, op0=ALU.mult, op1=ALU.add)
 
         nc.vector.tensor_scalar(
             out=xc[:, 0:X_HEAD, :], in0=xc[:, 0:X_HEAD, :], scalar1=-4.0, scalar2=4.0, op0=ALU.max, op1=ALU.min
@@ -144,40 +143,46 @@ def tile_kanlinearnores_t_kernel(tc, x, spline_weight, grad_out, out):
             )
             nc.scalar.activation(out=bw[:], in_=bw[:], func=ACT.Abs, bias=-2.0, scale=1.0)
             w = two.tile([P, 2, n, IN], F32, name="w")
-            aw = two.tile([P, 2, n, IN], F32, name="aw")
+            aw = two.tile([P, n, IN], F32, name="aw")
             nc.scalar.activation(out=w[:], in_=bw[:], func=ACT.Identity, bias=-1.25, scale=1.25)
-            nc.scalar.activation(out=aw[:], in_=bw[:], func=ACT.Abs, bias=-1.0, scale=1.0)
+            nc.scalar.activation(out=aw[:], in_=bw[:, 0, :, :], func=ACT.Abs, bias=-1.0, scale=1.0)
             st["w", c] = (w, aw)
 
-        def products(c):
+        def mx(c, j):
             g_codes, g_scales = st["codes", c]
+            pm = psum_m.tile([P, K], F32, name="pm")
+            nc.tensor.matmul_mx(
+                out=pm[:],
+                lhsT=g_codes[:, j * P : (j + 1) * P].bitcast(E5X4),
+                lhsT_scale=g_scales[:, j * P : (j + 1) * P],
+                rhs=w_codes[:].bitcast(E4X4),
+                rhs_scale=w_scales[:],
+                start=True,
+                stop=True,
+            )
+            st["pm", c, j] = pm
+
+        def products(c):
             ab = st["ab", c]
             tm = two.tile([P, SIZES[c], K], F32, name="tm")
             st["tm", c] = tm
             for j in range(SIZES[c]):
-                pm = psum_m.tile([P, K], F32, name="pm")
-                nc.tensor.matmul_mx(
-                    out=pm[:],
-                    lhsT=g_codes[:, j * P : (j + 1) * P].bitcast(E5X4),
-                    lhsT_scale=g_scales[:, j * P : (j + 1) * P],
-                    rhs=w_codes[:].bitcast(E4X4),
-                    rhs_scale=w_scales[:],
-                    start=True,
-                    stop=True,
-                )
                 nc.vector.scalar_tensor_tensor(
                     out=tm[:, j, :],
                     in0=ab[:, j, :, :].rearrange("p g i -> p (g i)"),
                     scalar=2.0,
-                    in1=pm[:],
+                    in1=st["pm", c, j][:],
                     op0=ALU.is_lt,
                     op1=ALU.mult,
                 )
+                if j + AHEAD < SIZES[c]:
+                    mx(c, j + AHEAD)
 
         def fold(c):
             tm = st["tm", c]
             s = two.tile([P, SIZES[c], K // 2], F32, name="s")
-            nc.gpsimd.tensor_tensor(out=s[:], in0=tm[:, :, 0 : K // 2], in1=tm[:, :, K // 2 : K], op=ALU.add)
+            eng = nc.vector if c == NCH - 1 else nc.gpsimd
+            eng.tensor_tensor(out=s[:], in0=tm[:, :, 0 : K // 2], in1=tm[:, :, K // 2 : K], op=ALU.add)
             st["s", c] = s
 
         def total(c):
@@ -188,7 +193,7 @@ def tile_kanlinearnores_t_kernel(tc, x, spline_weight, grad_out, out):
                 out=po[:], lhsT=ident[:], rhs=t[:, 0, :, :].rearrange("p c i -> p (c i)"), start=False, stop=False
             )
             nc.tensor.matmul(
-                out=po[:], lhsT=ident_neg[:], rhs=t[:, 1, :, :].rearrange("p c i -> p (c i)"), start=False, stop=True
+                out=po[:], lhsT=ident[:], rhs=t[:, 1, :, :].rearrange("p c i -> p (c i)"), start=False, stop=True
             )
             st["po", c] = po
 
@@ -206,8 +211,13 @@ def tile_kanlinearnores_t_kernel(tc, x, spline_weight, grad_out, out):
                 fold(d)
             if live(k):
                 products(k)
+            if live(k + 1):
+                quantise(k + 1)
             if live(k + 2):
                 transposes(k + 2)
+            if live(k + 1):
+                for j in range(min(AHEAD, SIZES[k + 1])):
+                    mx(k + 1, j)
             if live(k - 2):
                 total(k - 2)
             if live(k + 1) and k + 1 > 0:
@@ -232,7 +242,12 @@ def tile_kanlinearnores_t_kernel(tc, x, spline_weight, grad_out, out):
                 u = three.tile([P, n, IN], F32, name="u")
                 t = three.tile([P, 2, n, IN], F32, name="t")
                 st["ut", d] = (u, t)
-                nc.vector.scalar_tensor_tensor(out=ng[:], in0=aw[:], scalar=-2.0, in1=w[:], op0=ALU.add, op1=ALU.mult)
+                nc.vector.scalar_tensor_tensor(
+                    out=ng[:, 0, :, :], in0=aw[:], scalar=-2.0, in1=w[:, 0, :, :], op0=ALU.add, op1=ALU.mult
+                )
+                nc.vector.scalar_tensor_tensor(
+                    out=ng[:, 1, :, :], in0=aw[:], scalar=1.0, in1=w[:, 1, :, :], op0=ALU.add, op1=ALU.mult
+                )
                 nc.vector.tensor_tensor(out=dl[:], in0=first, in1=second, op=ALU.subtract)
                 nc.vector.tensor_tensor(out=sg[:], in0=first, in1=second, op=ALU.add)
                 nc.vector.scalar_tensor_tensor(
@@ -240,7 +255,4 @@ def tile_kanlinearnores_t_kernel(tc, x, spline_weight, grad_out, out):
                 )
                 nc.vector.tensor_tensor(out=t[:], in0=dl[:], in1=ng[:], op=ALU.mult)
                 nc.vector.tensor_tensor(out=ss[:], in0=sg[:, 0, :, :], in1=sg[:, 1, :, :], op=ALU.subtract)
-            if live(k + 1):
-                quantise(k + 1)
-            if live(d):
                 nc.vector.tensor_tensor(out=u[:], in0=ss[:], in1=pi[:], op=ALU.mult)

@@ -16,12 +16,13 @@ P = 128
 B, IN, OUT, NB = 8192, 64, 512, 8
 K = IN * NB
 NT = B // P
-SIZES = [4,4,4,4,4,4,4,4,4,4,4,4,4,4,4,2,2]
+SIZES = [2,2,4,8,8,8,8,8,8,4,2,2]
 NCH = len(SIZES)
 STARTS = [sum(SIZES[:c]) for c in range(NCH)]
 X_HEAD = 8
 ORDER = [0, 3, 2, 1, 4, 7, 6, 5]
 WAVE_PLANES = (1, 4)
+VECTOR_FOLDS = {2:2,4:2,8:1}
 AHEAD = 3
 G_BUFS = 4
 
@@ -177,13 +178,24 @@ def tile_kanlinearnores_t_kernel(tc, x, spline_weight, grad_out, out):
                 )
                 if j + AHEAD < SIZES[c]:
                     mx(c, j + AHEAD)
+                if j == 0:
+                    fold(c, 0, min(1, pool_end(c)), nc.gpsimd)
+                    if live(c - 1):
+                        fold(c - 1, 1, pool_end(c - 1), nc.gpsimd)
 
-        def fold(c):
+        def fold(c, j0, j1, eng):
+            if j0 >= j1:
+                return
+            if ("s", c) not in st:
+                s_new = two.tile([P, SIZES[c], K // 2], F32, name="s")
+                st["s", c] = s_new
             tm = st["tm", c]
-            s = two.tile([P, SIZES[c], K // 2], F32, name="s")
-            eng = nc.vector if c == NCH - 1 else nc.gpsimd
-            eng.tensor_tensor(out=s[:], in0=tm[:, :, 0 : K // 2], in1=tm[:, :, K // 2 : K], op=ALU.add)
-            st["s", c] = s
+            eng.tensor_tensor(
+                out=st["s", c][:, j0:j1, :], in0=tm[:, j0:j1, 0 : K // 2], in1=tm[:, j0:j1, K // 2 : K], op=ALU.add
+            )
+
+        def pool_end(c):
+            return SIZES[c] - VECTOR_FOLDS[SIZES[c]]
 
         def total(c):
             u, t = st["ut", c]
@@ -207,19 +219,19 @@ def tile_kanlinearnores_t_kernel(tc, x, spline_weight, grad_out, out):
             if live(k + G_BUFS - 1) and k + G_BUFS - 1 >= G_BUFS:
                 load(k + G_BUFS - 1)
             d = k - 1
-            if live(d):
-                fold(d)
+            if d == NCH - 1:
+                fold(d, 1, pool_end(d), nc.vector)
             if live(k):
                 products(k)
             if live(k + 1):
                 quantise(k + 1)
             if live(k + 2):
                 transposes(k + 2)
+            if live(k - 2):
+                total(k - 2)
             if live(k + 1):
                 for j in range(min(AHEAD, SIZES[k + 1])):
                     mx(k + 1, j)
-            if live(k - 2):
-                total(k - 2)
             if live(k + 1) and k + 1 > 0:
                 distances(k + 1)
             if live(k):
@@ -256,3 +268,5 @@ def tile_kanlinearnores_t_kernel(tc, x, spline_weight, grad_out, out):
                 nc.vector.tensor_tensor(out=t[:], in0=dl[:], in1=ng[:], op=ALU.mult)
                 nc.vector.tensor_tensor(out=ss[:], in0=sg[:, 0, :, :], in1=sg[:, 1, :, :], op=ALU.subtract)
                 nc.vector.tensor_tensor(out=u[:], in0=ss[:], in1=pi[:], op=ALU.mult)
+            if live(k):
+                fold(k, pool_end(k), SIZES[k], nc.vector)

@@ -22,7 +22,7 @@ STARTS = [sum(SIZES[:c]) for c in range(NCH)]
 X_HEAD = 8
 ORDER = [0, 3, 2, 1, 4, 7, 6, 5]
 WAVE_PLANES = (1, 4)
-VECTOR_FOLDS = {2:2,4:2,8:1}
+VECTOR_FOLDS = 1
 AHEAD = 3
 G_BUFS = 4
 
@@ -81,17 +81,23 @@ def tile_kanlinearnores_t_kernel(tc, x, spline_weight, grad_out, out):
         )
         w_grp = keep.tile([P, K, 4], BF16, align_bytes=64)
         w_view = w_raw[:].rearrange("p t (i g) -> p g i t", g=NB)
-        for pos in range(NB):
+        for pos in range(NB // 2):
             nc.vector.tensor_copy(out=w_grp[:, pos * IN : (pos + 1) * IN, :], in_=w_view[:, ORDER[pos], :, :])
+        for pos in range(NB // 2, NB):
+            nc.gpsimd.tensor_scalar(
+                out=w_grp[:, pos * IN : (pos + 1) * IN, :],
+                in0=w_view[:, ORDER[pos], :, :],
+                scalar1=1.0,
+                scalar2=0.0,
+                op0=ALU.mult,
+                op1=ALU.add,
+            )
         w_codes = keep.tile([P, K], U32, align_bytes=64)
         w_scales = keep.tile([P, K], U8, align_bytes=64)
         nc.vector.quantize_mx(
             out=w_codes[:].bitcast(E4X4),
             scales=w_scales[:],
             in_=w_grp[:].rearrange("p c t -> p (c t)"),
-        )
-        nc.vector.tensor_scalar(
-            out=xc[:, X_HEAD:NT, :], in0=xc[:, X_HEAD:NT, :], scalar1=-4.0, scalar2=4.0, op0=ALU.max, op1=ALU.min
         )
 
         def transposes(c):
@@ -178,10 +184,6 @@ def tile_kanlinearnores_t_kernel(tc, x, spline_weight, grad_out, out):
                 )
                 if j + AHEAD < SIZES[c]:
                     mx(c, j + AHEAD)
-                if j == 0:
-                    fold(c, 0, min(1, pool_end(c)), nc.gpsimd)
-                    if live(c - 1):
-                        fold(c - 1, 1, pool_end(c - 1), nc.gpsimd)
 
         def fold(c, j0, j1, eng):
             if j0 >= j1:
@@ -195,7 +197,7 @@ def tile_kanlinearnores_t_kernel(tc, x, spline_weight, grad_out, out):
             )
 
         def pool_end(c):
-            return SIZES[c] - VECTOR_FOLDS[SIZES[c]]
+            return 0 if c == NCH - 1 else SIZES[c] - VECTOR_FOLDS
 
         def total(c):
             u, t = st["ut", c]
@@ -219,12 +221,14 @@ def tile_kanlinearnores_t_kernel(tc, x, spline_weight, grad_out, out):
             if live(k + G_BUFS - 1) and k + G_BUFS - 1 >= G_BUFS:
                 load(k + G_BUFS - 1)
             d = k - 1
-            if d == NCH - 1:
-                fold(d, 1, pool_end(d), nc.vector)
             if live(k):
                 products(k)
             if live(k + 1):
                 quantise(k + 1)
+            if k == 0:
+                nc.vector.tensor_scalar(
+                    out=xc[:, X_HEAD:NT, :], in0=xc[:, X_HEAD:NT, :], scalar1=-4.0, scalar2=4.0, op0=ALU.max, op1=ALU.min
+                )
             if live(k + 2):
                 transposes(k + 2)
             if live(k - 2):
@@ -266,7 +270,11 @@ def tile_kanlinearnores_t_kernel(tc, x, spline_weight, grad_out, out):
                     out=pi[:], in0=w[:, 0, :, :], scalar=1.6, in1=w[:, 1, :, :], op0=ALU.mult, op1=ALU.mult
                 )
                 nc.vector.tensor_tensor(out=t[:], in0=dl[:], in1=ng[:], op=ALU.mult)
-                nc.vector.tensor_tensor(out=ss[:], in0=sg[:, 0, :, :], in1=sg[:, 1, :, :], op=ALU.subtract)
-                nc.vector.tensor_tensor(out=u[:], in0=ss[:], in1=pi[:], op=ALU.mult)
             if live(k):
                 fold(k, pool_end(k), SIZES[k], nc.vector)
+            if live(d):
+                nc.vector.tensor_tensor(out=ss[:], in0=sg[:, 0, :, :], in1=sg[:, 1, :, :], op=ALU.subtract)
+                eng = nc.vector if d == NCH - 1 else nc.gpsimd
+                eng.tensor_tensor(out=u[:], in0=ss[:], in1=pi[:], op=ALU.mult)
+            if live(k):
+                fold(k, 0, pool_end(k), nc.gpsimd)

@@ -22,7 +22,7 @@ STARTS = [sum(SIZES[:c]) for c in range(NCH)]
 X_HEAD = 8
 ORDER = [0, 3, 2, 1, 4, 7, 6, 5]
 WAVE_PLANES = (1, 4)
-VECTOR_FOLDS = 1
+VECTOR_FOLDS = {2:2,4:2,8:1}
 AHEAD = 3
 G_BUFS = 4
 
@@ -184,6 +184,10 @@ def tile_kanlinearnores_t_kernel(tc, x, spline_weight, grad_out, out):
                 )
                 if j + AHEAD < SIZES[c]:
                     mx(c, j + AHEAD)
+                if j == 0:
+                    fold(c, 0, min(1, pool_end(c)), nc.gpsimd)
+                    if live(c - 1):
+                        fold(c - 1, 1, pool_end(c - 1), nc.gpsimd)
 
         def fold(c, j0, j1, eng):
             if j0 >= j1:
@@ -197,7 +201,7 @@ def tile_kanlinearnores_t_kernel(tc, x, spline_weight, grad_out, out):
             )
 
         def pool_end(c):
-            return 0 if c == NCH - 1 else SIZES[c] - VECTOR_FOLDS
+            return SIZES[c] - VECTOR_FOLDS[SIZES[c]]
 
         def total(c):
             u, t = st["ut", c]
@@ -221,6 +225,8 @@ def tile_kanlinearnores_t_kernel(tc, x, spline_weight, grad_out, out):
             if live(k + G_BUFS - 1) and k + G_BUFS - 1 >= G_BUFS:
                 load(k + G_BUFS - 1)
             d = k - 1
+            if d == NCH - 1:
+                fold(d, 1, pool_end(d), nc.vector)
             if live(k):
                 products(k)
             if live(k + 1):
@@ -269,12 +275,8 @@ def tile_kanlinearnores_t_kernel(tc, x, spline_weight, grad_out, out):
                 nc.vector.scalar_tensor_tensor(
                     out=pi[:], in0=w[:, 0, :, :], scalar=1.6, in1=w[:, 1, :, :], op0=ALU.mult, op1=ALU.mult
                 )
+                nc.vector.tensor_tensor(out=ss[:], in0=sg[:, 0, :, :], in1=sg[:, 1, :, :], op=ALU.subtract)
                 nc.vector.tensor_tensor(out=t[:], in0=dl[:], in1=ng[:], op=ALU.mult)
+                nc.vector.tensor_tensor(out=u[:], in0=ss[:], in1=pi[:], op=ALU.mult)
             if live(k):
                 fold(k, pool_end(k), SIZES[k], nc.vector)
-            if live(d):
-                nc.vector.tensor_tensor(out=ss[:], in0=sg[:, 0, :, :], in1=sg[:, 1, :, :], op=ALU.subtract)
-                eng = nc.vector if d == NCH - 1 else nc.gpsimd
-                eng.tensor_tensor(out=u[:], in0=ss[:], in1=pi[:], op=ALU.mult)
-            if live(k):
-                fold(k, 0, pool_end(k), nc.gpsimd)

@@ -16,15 +16,14 @@ P = 128
 B, IN, OUT, NB = 8192, 64, 512, 8
 K = IN * NB
 NT = B // P
-SIZES = [2,2,4,8,8,8,8,8,8,4,2,2]
-NCH = len(SIZES)
-STARTS = [sum(SIZES[:c]) for c in range(NCH)]
+NPAIR = NT // 2
+LOADS = [2, 2, 4] + [8] * 7
+GROUPS = [1, 1, 2] + [4] * 7
+BLOCK = 4
 X_HEAD = 8
-ORDER = [0, 3, 2, 1, 4, 7, 6, 5]
-WAVE_PLANES = (1, 4)
-VECTOR_FOLDS = {2:2,4:2,8:1}
-AHEAD = 3
 G_BUFS = 4
+NEGATED = (2, 3, 6, 7)
+DIFFS = ((0, 4, 2, 6), (1, 5, 3, 7), (0, 4, 3, 7))
 
 FLOPS = 2 * B * OUT * K
 
@@ -36,28 +35,37 @@ def tile_kanlinearnores_t_kernel(tc, x, spline_weight, grad_out, out):
     o_v = out.rearrange("(p t) i -> p t i", t=NT)
     w2 = spline_weight.rearrange("o i g -> o (i g)")
 
+    load_start = [sum(LOADS[:n]) for n in range(len(LOADS))]
+    group_start = [sum(GROUPS[:n]) for n in range(len(GROUPS))]
+    load_of = {}
+    for n, s in enumerate(load_start):
+        for j in range(LOADS[n]):
+            load_of[s + j] = (n, j)
+    group_of = {}
+    for n, s in enumerate(group_start):
+        for q in range(GROUPS[n]):
+            group_of[s + q] = (n, q)
+
     with ExitStack() as ctx:
         ctx.enter_context(tc.manual_schedule())
         keep = ctx.enter_context(tc.tile_pool(name="keep", bufs=1))
         two = ctx.enter_context(tc.tile_pool(name="two", bufs=2))
         three = ctx.enter_context(tc.tile_pool(name="three", bufs=3))
         gin = ctx.enter_context(tc.tile_pool(name="gin", bufs=G_BUFS))
-        psum_t = ctx.enter_context(tc.psum_pool(name="psum_t", bufs=4))
-        psum_m = ctx.enter_context(tc.psum_pool(name="psum_m", bufs=3))
-        psum_o = ctx.enter_context(tc.psum_pool(name="psum_o", bufs=1))
+        psum_t = ctx.enter_context(tc.psum_pool(name="psum_t", bufs=2))
+        psum_x = ctx.enter_context(tc.psum_pool(name="psum_x", bufs=1))
+        psum_m = ctx.enter_context(tc.psum_pool(name="psum_m", bufs=2))
+        psum_e = ctx.enter_context(tc.psum_pool(name="psum_e", bufs=3))
 
         st = {}
 
-        def live(c):
-            return 0 <= c < NCH
+        def live(q):
+            return 0 <= q < NPAIR
 
-        def span(c):
-            return slice(STARTS[c], STARTS[c] + SIZES[c])
-
-        def load(c):
-            g_sb = gin.tile([P, SIZES[c], OUT], BF16, name="g_sb")
-            nc.sync.dma_start(out=g_sb[:], in_=g_v[:, span(c), :])
-            st["g", c] = g_sb
+        def load(n):
+            g_sb = gin.tile([P, LOADS[n], OUT], BF16, name="g_sb")
+            nc.sync.dma_start(out=g_sb[:], in_=g_v[:, load_start[n] : load_start[n] + LOADS[n], :])
+            st["g", n] = g_sb
 
         w_raw = keep.tile([P, 4, K], BF16)
         for u in range(2):
@@ -70,24 +78,25 @@ def tile_kanlinearnores_t_kernel(tc, x, spline_weight, grad_out, out):
         load(0)
         load(1)
         nc.sync.dma_start(out=xc[:, X_HEAD:NT, :], in_=x_v[:, X_HEAD:NT, :])
-        for c in range(2, G_BUFS):
-            load(c)
+        for n in range(2, G_BUFS):
+            load(n)
 
         ident = keep.tile([P, P], F32)
         make_identity(nc, ident[:])
+        ident_b = keep.tile([P, P], BF16)
+        make_identity(nc, ident_b[:])
 
         nc.vector.tensor_scalar(
             out=xc[:, 0:X_HEAD, :], in0=xc[:, 0:X_HEAD, :], scalar1=-4.0, scalar2=4.0, op0=ALU.max, op1=ALU.min
         )
         w_grp = keep.tile([P, K, 4], BF16, align_bytes=64)
         w_view = w_raw[:].rearrange("p t (i g) -> p g i t", g=NB)
-        for pos in range(NB // 2):
-            nc.vector.tensor_copy(out=w_grp[:, pos * IN : (pos + 1) * IN, :], in_=w_view[:, ORDER[pos], :, :])
-        for pos in range(NB // 2, NB):
-            nc.gpsimd.tensor_scalar(
-                out=w_grp[:, pos * IN : (pos + 1) * IN, :],
-                in0=w_view[:, ORDER[pos], :, :],
-                scalar1=1.0,
+        for g in range(NB):
+            eng = nc.vector if g < NB // 2 else nc.gpsimd
+            eng.tensor_scalar(
+                out=w_grp[:, g * IN : (g + 1) * IN, :],
+                in0=w_view[:, g, :, :],
+                scalar1=-1.0 if g in NEGATED else 1.0,
                 scalar2=0.0,
                 op0=ALU.mult,
                 op1=ALU.add,
@@ -100,183 +109,210 @@ def tile_kanlinearnores_t_kernel(tc, x, spline_weight, grad_out, out):
             in_=w_grp[:].rearrange("p c t -> p (c t)"),
         )
 
-        def transposes(c):
-            n = SIZES[c]
-            g32 = st["g", c][:].bitcast(F32)
-            pts = []
-            for h in range(n // 2):
-                pt = psum_t.tile([P, 2, 2, P], F32, name="pt")
-                for j in range(2):
-                    for u in range(2):
-                        nc.tensor.transpose(pt[:, j, u, :], g32[:, 2 * h + j, P * u : P * u + P], ident[:])
-                pts.append(pt)
-            st["pts", c] = pts
+        def x_transposes(b):
+            xt = psum_x.tile([P, BLOCK, P], BF16, name="xt")
+            for q in range(BLOCK):
+                t = 2 * (BLOCK * b + q)
+                nc.tensor.transpose(xt[:, q, :], xc[:, t : t + 2, :].rearrange("p t i -> p (t i)"), ident_b[:])
+            st["xt", b] = xt
 
-        def regroup(c):
-            n = SIZES[c]
-            grp = two.tile([P, n * P, 2], F32, name="grp", align_bytes=64)
-            st["grp", c] = grp
-            for h in range(n // 2):
-                nc.scalar.copy(
-                    out=grp[:, 2 * h * P : (2 * h + 2) * P, :].rearrange("p (j r) u -> p j r u", j=2),
-                    in_=st["pts", c][h][:].rearrange("p j u r -> p j r u"),
+        def chain_a(n):
+            w = GROUPS[n] * P
+            b, off = divmod(group_start[n], BLOCK)
+            xt = st["xt", b][:, off : off + GROUPS[n], :].rearrange("p q t -> p (q t)")
+            a = two.tile([P, 2, w], F32, name="a")
+            for k in range(2):
+                nc.scalar.activation(out=a[:, k, :], in_=xt, func=ACT.Abs, bias=0.5 - k, scale=2.5)
+            nc.scalar.activation(out=a[:], in_=a[:], func=ACT.Abs, bias=-2.0, scale=1.0)
+            st["a", n] = a
+
+        def chain_b(n):
+            w = GROUPS[n] * P
+            bh = two.tile([P, 2, w], F32, name="bh")
+            nc.scalar.activation(out=bh[:], in_=st["a", n][:], func=ACT.Abs, bias=-1.0, scale=0.5)
+            hq = two.tile([P, 2, w], F32, name="hq")
+            nc.scalar.activation(out=hq[:], in_=bh[:], func=ACT.Abs, bias=-0.25, scale=0.5)
+            nz = two.tile([P, 2, w], F32, name="nz")
+            nc.gpsimd.tensor_scalar(out=nz[:], in0=bh[:], scalar1=-2.0, scalar2=1.0, op0=ALU.mult, op1=ALU.add)
+            r = two.tile([P, 2, w], F32, name="r")
+            for k in range(2):
+                nc.gpsimd.tensor_tensor(out=r[:, k, :], in0=bh[:, 1 - k, :], in1=hq[:, k, :], op=ALU.subtract)
+            cf = two.tile([P, GROUPS[n], 3, P], F32, name="cf")
+            nc.gpsimd.tensor_tensor(
+                out=cf[:, :, 0:2, :].rearrange("p q e t -> p e q t"),
+                in0=nz[:].rearrange("p e (q t) -> p e q t", t=P),
+                in1=r[:].rearrange("p e (q t) -> p e q t", t=P),
+                op=ALU.mult,
+            )
+            nc.gpsimd.tensor_tensor(
+                out=cf[:, :, 2, :],
+                in0=nz[:, 0, :].rearrange("p (q t) -> p q t", t=P),
+                in1=nz[:, 1, :].rearrange("p (q t) -> p q t", t=P),
+                op=ALU.mult,
+            )
+            st["cf", n] = cf
+
+        def distances(n, planes):
+            t0 = 2 * group_start[n]
+            if ("ab", n) not in st:
+                ab_new = two.tile([P, NB, 2 * GROUPS[n], IN], F32, name="ab")
+                st["ab", n] = ab_new
+            for g in planes:
+                nc.scalar.activation(
+                    out=st["ab", n][:, g, :, :],
+                    in_=xc[:, t0 : t0 + 2 * GROUPS[n], :],
+                    func=ACT.Abs,
+                    bias=3.5 - g,
+                    scale=2.5,
                 )
 
-        def quantise(c):
-            n = SIZES[c]
-            g_codes = two.tile([P, n * P], U32, name="g_codes", align_bytes=64)
-            g_scales = two.tile([P, n * P], U8, name="g_scales", align_bytes=64)
+        def x_work(n, part):
+            if part == 0:
+                chain_a(n)
+            elif part == 1:
+                chain_b(n)
+            elif part == 2:
+                distances(n, range(0, NB // 2))
+            else:
+                distances(n, range(NB // 2, NB))
+
+        def g_transposes(q):
+            n, off = load_of[2 * q]
+            g32 = st["g", n][:].bitcast(F32)
+            pt = psum_t.tile([P, 2, 2, P], F32, name="pt")
+            for j in range(2):
+                for u in range(2):
+                    nc.tensor.transpose(pt[:, j, u, :], g32[:, off + j, P * u : P * u + P], ident[:])
+            st["pt", q] = pt
+            if off + 2 == LOADS[n] and n + G_BUFS < len(LOADS):
+                load(n + G_BUFS)
+
+        def regroup(q):
+            grp = three.tile([P, 2 * P, 2], F32, name="grp", align_bytes=64)
+            nc.vector.tensor_copy(
+                out=grp[:].rearrange("p (j r) u -> p j r u", j=2),
+                in_=st["pt", q][:].rearrange("p j u r -> p j r u"),
+            )
+            st["grp", q] = grp
+
+        def quantise(q):
+            g_codes = three.tile([P, 2 * P], U32, name="g_codes", align_bytes=64)
+            g_scales = three.tile([P, 2 * P], U8, name="g_scales", align_bytes=64)
             nc.vector.quantize_mx(
                 out=g_codes[:].bitcast(E5X4),
                 scales=g_scales[:],
-                in_=st["grp", c][:].rearrange("p r u -> p (r u)").bitcast(BF16),
+                in_=st["grp", q][:].rearrange("p r u -> p (r u)").bitcast(BF16),
             )
-            st["codes", c] = (g_codes, g_scales)
+            st["codes", q] = (g_codes, g_scales)
 
-        def distances(c):
-            ab = two.tile([P, SIZES[c], NB, IN], F32, name="ab")
-            st["ab", c] = ab
-            for pos in range(NB):
-                nc.scalar.activation(
-                    out=ab[:, :, pos, :], in_=xc[:, span(c), :], func=ACT.Abs, bias=3.5 - ORDER[pos], scale=2.5
+        def mx(q):
+            g_codes, g_scales = st["codes", q]
+            for j in range(2):
+                pm = psum_m.tile([P, K], F32, name="pm")
+                nc.tensor.matmul_mx(
+                    out=pm[:],
+                    lhsT=g_codes[:, j * P : (j + 1) * P].bitcast(E5X4),
+                    lhsT_scale=g_scales[:, j * P : (j + 1) * P],
+                    rhs=w_codes[:].bitcast(E4X4),
+                    rhs_scale=w_scales[:],
+                    start=True,
+                    stop=True,
                 )
+                st["pm", q, j] = pm
 
-        def waves(c):
-            n = SIZES[c]
-            ab = st["ab", c]
-            bw = two.tile([P, 2, n, IN], F32, name="bw")
-            nc.scalar.activation(
-                out=bw[:], in_=ab[:, :, 1:5:3, :].rearrange("p c j i -> p j c i"), func=ACT.Abs, bias=-2.0, scale=1.0
-            )
-            nc.scalar.activation(out=bw[:], in_=bw[:], func=ACT.Abs, bias=-2.0, scale=1.0)
-            w = two.tile([P, 2, n, IN], F32, name="w")
-            aw = two.tile([P, n, IN], F32, name="aw")
-            nc.scalar.activation(out=w[:], in_=bw[:], func=ACT.Identity, bias=-1.25, scale=1.25)
-            nc.scalar.activation(out=aw[:], in_=bw[:, 0, :, :], func=ACT.Abs, bias=-1.0, scale=1.0)
-            st["w", c] = (w, aw)
-
-        def mx(c, j):
-            g_codes, g_scales = st["codes", c]
-            pm = psum_m.tile([P, K], F32, name="pm")
-            nc.tensor.matmul_mx(
-                out=pm[:],
-                lhsT=g_codes[:, j * P : (j + 1) * P].bitcast(E5X4),
-                lhsT_scale=g_scales[:, j * P : (j + 1) * P],
-                rhs=w_codes[:].bitcast(E4X4),
-                rhs_scale=w_scales[:],
-                start=True,
-                stop=True,
-            )
-            st["pm", c, j] = pm
-
-        def products(c):
-            ab = st["ab", c]
-            tm = two.tile([P, SIZES[c], K], F32, name="tm")
-            st["tm", c] = tm
-            for j in range(SIZES[c]):
+        def products(q):
+            n, off = group_of[q]
+            if off == 0:
+                tm_new = two.tile([P, NB, 2 * GROUPS[n], IN], F32, name="tm")
+                st["tm", n] = tm_new
+            for j in range(2):
                 nc.vector.scalar_tensor_tensor(
-                    out=tm[:, j, :],
-                    in0=ab[:, j, :, :].rearrange("p g i -> p (g i)"),
+                    out=st["tm", n][:, :, 2 * off + j, :],
+                    in0=st["ab", n][:, :, 2 * off + j, :],
                     scalar=2.0,
-                    in1=st["pm", c, j][:],
+                    in1=st["pm", q, j][:].rearrange("p (g i) -> p g i", g=NB),
                     op0=ALU.is_lt,
                     op1=ALU.mult,
                 )
-                if j + AHEAD < SIZES[c]:
-                    mx(c, j + AHEAD)
-                if j == 0:
-                    fold(c, 0, min(1, pool_end(c)), nc.gpsimd)
-                    if live(c - 1):
-                        fold(c - 1, 1, pool_end(c - 1), nc.gpsimd)
 
-        def fold(c, j0, j1, eng):
-            if j0 >= j1:
-                return
-            if ("s", c) not in st:
-                s_new = two.tile([P, SIZES[c], K // 2], F32, name="s")
-                st["s", c] = s_new
-            tm = st["tm", c]
-            eng.tensor_tensor(
-                out=st["s", c][:, j0:j1, :], in0=tm[:, j0:j1, 0 : K // 2], in1=tm[:, j0:j1, K // 2 : K], op=ALU.add
-            )
+        def e_sums(q):
+            n, off = group_of[q]
+            eo = psum_e.tile([P, 4, P], F32, name="eo")
+            for e, planes in enumerate(DIFFS):
+                for m, g in enumerate(planes):
+                    nc.tensor.matmul(
+                        out=eo[:, e, :],
+                        lhsT=st["tm", n][:, g, 2 * off : 2 * off + 2, :].rearrange("p t i -> p (t i)"),
+                        rhs=ident[:],
+                        start=(m == 0),
+                        stop=(m == len(planes) - 1),
+                        is_transpose=True,
+                    )
+            st["eo", q] = eo
 
-        def pool_end(c):
-            return SIZES[c] - VECTOR_FOLDS[SIZES[c]]
+        def weigh(q):
+            n, off = group_of[q]
+            pr = three.tile([P, 3, P], F32, name="pr")
+            nc.vector.tensor_tensor(out=pr[:], in0=st["eo", q][:, 0:3, :], in1=st["cf", n][:, off, :, :], op=ALU.mult)
+            st["pr", q] = pr
 
-        def total(c):
-            u, t = st["ut", c]
-            po = psum_o.tile([P, SIZES[c] * IN], F32, name="po")
-            nc.tensor.matmul(out=po[:], lhsT=ident[:], rhs=u[:].rearrange("p c i -> p (c i)"), start=True, stop=False)
-            nc.tensor.matmul(
-                out=po[:], lhsT=ident[:], rhs=t[:, 0, :, :].rearrange("p c i -> p (c i)"), start=False, stop=False
-            )
-            nc.tensor.matmul(
-                out=po[:], lhsT=ident[:], rhs=t[:, 1, :, :].rearrange("p c i -> p (c i)"), start=False, stop=True
-            )
-            st["po", c] = po
+        def o_sums(q):
+            for e in range(3):
+                nc.tensor.matmul(
+                    out=st["eo", q][:, 3, :],
+                    lhsT=st["pr", q][:, e, :],
+                    rhs=ident[:],
+                    start=(e == 0),
+                    stop=(e == 2),
+                    is_transpose=True,
+                )
 
-        def store(c):
-            o = two.tile([P, SIZES[c] * IN], F32, name="o")
-            nc.scalar.copy(out=o[:], in_=st["po", c][:])
-            nc.sync.dma_start(out=o_v[:, span(c), :], in_=o[:].rearrange("p (c i) -> p c i", i=IN))
+        def copy_out(q):
+            n, off = group_of[q]
+            if off == 0:
+                o_new = two.tile([P, GROUPS[n] * P], F32, name="o")
+                st["o", n] = o_new
+            o = st["o", n]
+            nc.scalar.activation(out=o[:, off * P : (off + 1) * P], in_=st["eo", q][:, 3, :], func=ACT.Copy, scale=5.0)
+            if off == GROUPS[n] - 1:
+                t0 = 2 * group_start[n]
+                nc.sync.dma_start(
+                    out=o_v[:, t0 : t0 + 2 * GROUPS[n], :], in_=o[:].rearrange("p (t i) -> p t i", i=IN)
+                )
 
-        distances(0)
-        for k in range(-2, NCH + 2):
-            if live(k + G_BUFS - 1) and k + G_BUFS - 1 >= G_BUFS:
-                load(k + G_BUFS - 1)
-            d = k - 1
-            if d == NCH - 1:
-                fold(d, 1, pool_end(d), nc.vector)
-            if live(k):
-                products(k)
-            if live(k + 1):
-                quantise(k + 1)
-            if k == 0:
+        x_transposes(0)
+        for part in range(4):
+            x_work(0, part)
+        for q in range(-4, NPAIR + 2):
+            if live(q - 1):
+                e_sums(q - 1)
+            if live(q - 2):
+                o_sums(q - 2)
+            if live(q):
+                products(q)
+            if live(q + 1):
+                mx(q + 1)
+            if live(q + 4):
+                g_transposes(q + 4)
+            if live(q):
+                n, off = group_of[q]
+                nxt = n + 2
+                if off == GROUPS[n] - 1 and nxt < len(GROUPS) and group_start[nxt] % BLOCK == 0:
+                    x_transposes(group_start[nxt] // BLOCK)
+            if live(q - 1):
+                weigh(q - 1)
+            if live(q + 3):
+                regroup(q + 3)
+            if live(q + 2):
+                quantise(q + 2)
+            if q == -1:
                 nc.vector.tensor_scalar(
                     out=xc[:, X_HEAD:NT, :], in0=xc[:, X_HEAD:NT, :], scalar1=-4.0, scalar2=4.0, op0=ALU.max, op1=ALU.min
                 )
-            if live(k + 2):
-                transposes(k + 2)
-            if live(k - 2):
-                total(k - 2)
-            if live(k + 1):
-                for j in range(min(AHEAD, SIZES[k + 1])):
-                    mx(k + 1, j)
-            if live(k + 1) and k + 1 > 0:
-                distances(k + 1)
-            if live(k):
-                waves(k)
-            if live(k + 2):
-                regroup(k + 2)
-            if live(k - 2):
-                store(k - 2)
-            if live(d):
-                n = SIZES[d]
-                w, aw = st["w", d]
-                s = st["s", d]
-                first = s[:, :, 0 : 2 * IN].rearrange("p c (j i) -> p j c i", j=2)
-                second = s[:, :, 2 * IN : 4 * IN].rearrange("p c (j i) -> p j c i", j=2)
-                pi = keep.tile([P, n, IN], F32, name="pi")
-                ng = keep.tile([P, 2, n, IN], F32, name="ng")
-                sg = keep.tile([P, 2, n, IN], F32, name="sg")
-                dl = keep.tile([P, 2, n, IN], F32, name="dl")
-                ss = keep.tile([P, n, IN], F32, name="ss")
-                u = three.tile([P, n, IN], F32, name="u")
-                t = three.tile([P, 2, n, IN], F32, name="t")
-                st["ut", d] = (u, t)
-                nc.vector.scalar_tensor_tensor(
-                    out=ng[:, 0, :, :], in0=aw[:], scalar=-2.0, in1=w[:, 0, :, :], op0=ALU.add, op1=ALU.mult
-                )
-                nc.vector.scalar_tensor_tensor(
-                    out=ng[:, 1, :, :], in0=aw[:], scalar=1.0, in1=w[:, 1, :, :], op0=ALU.add, op1=ALU.mult
-                )
-                nc.vector.tensor_tensor(out=dl[:], in0=first, in1=second, op=ALU.subtract)
-                nc.vector.tensor_tensor(out=sg[:], in0=first, in1=second, op=ALU.add)
-                nc.vector.scalar_tensor_tensor(
-                    out=pi[:], in0=w[:, 0, :, :], scalar=1.6, in1=w[:, 1, :, :], op0=ALU.mult, op1=ALU.mult
-                )
-                nc.vector.tensor_tensor(out=ss[:], in0=sg[:, 0, :, :], in1=sg[:, 1, :, :], op=ALU.subtract)
-                nc.vector.tensor_tensor(out=t[:], in0=dl[:], in1=ng[:], op=ALU.mult)
-                nc.vector.tensor_tensor(out=u[:], in0=ss[:], in1=pi[:], op=ALU.mult)
-            if live(k):
-                fold(k, pool_end(k), SIZES[k], nc.vector)
+            if live(q):
+                n, off = group_of[q]
+                if n + 1 < len(GROUPS):
+                    for part in range(4 * off // GROUPS[n], 4 * (off + 1) // GROUPS[n]):
+                        x_work(n + 1, part)
+            if live(q - 2):
+                copy_out(q - 2)

@@ -286,12 +286,10 @@ def tile_kanlinearnores_t_kernel(tc, x, spline_weight, grad_out, out):
         for q in range(-4, NPAIR + 2):
             if live(q - 1):
                 e_sums(q - 1)
-            if live(q - 2):
-                o_sums(q - 2)
             if live(q):
                 products(q)
-            if live(q + 1):
-                mx(q + 1)
+            if live(q - 2):
+                o_sums(q - 2)
             if live(q + 4):
                 g_transposes(q + 4)
             if live(q):
@@ -299,12 +297,14 @@ def tile_kanlinearnores_t_kernel(tc, x, spline_weight, grad_out, out):
                 nxt = n + 2
                 if off == GROUPS[n] - 1 and nxt < len(GROUPS) and group_start[nxt] % BLOCK == 0:
                     x_transposes(group_start[nxt] // BLOCK)
-            if live(q - 1):
-                weigh(q - 1)
+            if live(q + 1):
+                mx(q + 1)
             if live(q + 3):
                 regroup(q + 3)
             if live(q + 2):
                 quantise(q + 2)
+            if live(q - 1):
+                weigh(q - 1)
             if q == -1:
                 nc.vector.tensor_scalar(
                     out=xc[:, X_HEAD:NT, :], in0=xc[:, X_HEAD:NT, :], scalar1=-4.0, scalar2=4.0, op0=ALU.max, op1=ALU.min

@@ -18,7 +18,7 @@ K = IN * NB
 NT = B // P
 NPAIR = NT // 2
 LOADS = [2, 2, 4] + [8] * 7
-GROUPS = [1, 1, 2] + [4] * 7
+GROUPS = [2, 2] + [4] * 7
 BLOCK = 4
 X_HEAD = 8
 G_BUFS = 4
@@ -55,7 +55,8 @@ def tile_kanlinearnores_t_kernel(tc, x, spline_weight, grad_out, out):
         psum_t = ctx.enter_context(tc.psum_pool(name="psum_t", bufs=2))
         psum_x = ctx.enter_context(tc.psum_pool(name="psum_x", bufs=1))
         psum_m = ctx.enter_context(tc.psum_pool(name="psum_m", bufs=2))
-        psum_e = ctx.enter_context(tc.psum_pool(name="psum_e", bufs=3))
+        psum_e = ctx.enter_context(tc.psum_pool(name="psum_e", bufs=2))
+        psum_o = ctx.enter_context(tc.psum_pool(name="psum_o", bufs=1))
 
         st = {}
 
@@ -237,7 +238,7 @@ def tile_kanlinearnores_t_kernel(tc, x, spline_weight, grad_out, out):
 
         def e_sums(q):
             n, off = group_of[q]
-            eo = psum_e.tile([P, 4, P], F32, name="eo")
+            eo = psum_e.tile([P, 3, P], F32, name="eo")
             for e, planes in enumerate(DIFFS):
                 for m, g in enumerate(planes):
                     nc.tensor.matmul(
@@ -253,13 +254,17 @@ def tile_kanlinearnores_t_kernel(tc, x, spline_weight, grad_out, out):
         def weigh(q):
             n, off = group_of[q]
             pr = three.tile([P, 3, P], F32, name="pr")
-            nc.vector.tensor_tensor(out=pr[:], in0=st["eo", q][:, 0:3, :], in1=st["cf", n][:, off, :, :], op=ALU.mult)
+            nc.vector.tensor_tensor(out=pr[:], in0=st["eo", q][:], in1=st["cf", n][:, off, :, :], op=ALU.mult)
             st["pr", q] = pr
 
         def o_sums(q):
+            n, off = group_of[q]
+            if off == 0:
+                ob_new = psum_o.tile([P, GROUPS[n], P], F32, name="ob")
+                st["ob", n] = ob_new
             for e in range(3):
                 nc.tensor.matmul(
-                    out=st["eo", q][:, 3, :],
+                    out=st["ob", n][:, off, :],
                     lhsT=st["pr", q][:, e, :],
                     rhs=ident[:],
                     start=(e == 0),
@@ -267,23 +272,18 @@ def tile_kanlinearnores_t_kernel(tc, x, spline_weight, grad_out, out):
                     is_transpose=True,
                 )
 
-        def copy_out(q):
-            n, off = group_of[q]
-            if off == 0:
-                o_new = two.tile([P, GROUPS[n] * P], F32, name="o")
-                st["o", n] = o_new
-            o = st["o", n]
-            nc.scalar.activation(out=o[:, off * P : (off + 1) * P], in_=st["eo", q][:, 3, :], func=ACT.Copy, scale=5.0)
-            if off == GROUPS[n] - 1:
-                t0 = 2 * group_start[n]
-                nc.sync.dma_start(
-                    out=o_v[:, t0 : t0 + 2 * GROUPS[n], :], in_=o[:].rearrange("p (t i) -> p t i", i=IN)
-                )
+        def copy_out(n):
+            o = two.tile([P, GROUPS[n] * P], F32, name="o")
+            nc.scalar.activation(out=o[:], in_=st["ob", n][:].rearrange("p q t -> p (q t)"), func=ACT.Copy, scale=5.0)
+            t0 = 2 * group_start[n]
+            nc.sync.dma_start(out=o_v[:, t0 : t0 + 2 * GROUPS[n], :], in_=o[:].rearrange("p (t i) -> p t i", i=IN))
 
         x_transposes(0)
         for part in range(4):
             x_work(0, part)
-        for q in range(-4, NPAIR + 2):
+        for q in range(-4, NPAIR + 3):
+            if live(q - 3) and group_of[q - 3][1] == GROUPS[group_of[q - 3][0]] - 1:
+                copy_out(group_of[q - 3][0])
             if live(q - 1):
                 e_sums(q - 1)
             if live(q):
@@ -314,5 +314,3 @@ def tile_kanlinearnores_t_kernel(tc, x, spline_weight, grad_out, out):
                 if n + 1 < len(GROUPS):
                     for part in range(4 * off // GROUPS[n], 4 * (off + 1) // GROUPS[n]):
                         x_work(n + 1, part)
-            if live(q - 2):
-                copy_out(q - 2)

from contextlib import ExitStack

import concourse.mybir as mybir
from concourse.masks import make_identity

F32 = mybir.dt.float32
BF16 = mybir.dt.bfloat16
U32 = mybir.dt.uint32
U8 = mybir.dt.uint8
E4X4 = mybir.dt.float8_e4m3fn_x4
E5X4 = mybir.dt.float8_e5m2_x4
ALU = mybir.AluOpType
ACT = mybir.ActivationFunctionType

P = 128
B, IN, OUT, NB = 8192, 64, 512, 8
K = IN * NB
NT = B // P
NPAIR = NT // 2
LOADS = [2, 2, 4] + [8] * 7
GROUPS = [2, 2] + [4] * 7
BLOCK = 4
X_HEAD = 8
G_BUFS = 4
NEGATED = (2, 3, 6, 7)
DIFFS = ((0, 4, 2, 6), (1, 5, 3, 7), (0, 4, 3, 7))

FLOPS = 2 * B * OUT * K


def tile_kanlinearnores_t_kernel(tc, x, spline_weight, grad_out, out):
    nc = tc.nc
    g_v = grad_out.rearrange("(p t) k -> p t k", t=NT)
    x_v = x.rearrange("(p t) i -> p t i", t=NT)
    o_v = out.rearrange("(p t) i -> p t i", t=NT)
    w2 = spline_weight.rearrange("o i g -> o (i g)")

    load_start = [sum(LOADS[:n]) for n in range(len(LOADS))]
    group_start = [sum(GROUPS[:n]) for n in range(len(GROUPS))]
    load_of = {}
    for n, s in enumerate(load_start):
        for j in range(LOADS[n]):
            load_of[s + j] = (n, j)
    group_of = {}
    for n, s in enumerate(group_start):
        for q in range(GROUPS[n]):
            group_of[s + q] = (n, q)

    with ExitStack() as ctx:
        ctx.enter_context(tc.manual_schedule())
        keep = ctx.enter_context(tc.tile_pool(name="keep", bufs=1))
        two = ctx.enter_context(tc.tile_pool(name="two", bufs=2))
        three = ctx.enter_context(tc.tile_pool(name="three", bufs=3))
        gin = ctx.enter_context(tc.tile_pool(name="gin", bufs=G_BUFS))
        psum_t = ctx.enter_context(tc.psum_pool(name="psum_t", bufs=2))
        psum_x = ctx.enter_context(tc.psum_pool(name="psum_x", bufs=1))
        psum_m = ctx.enter_context(tc.psum_pool(name="psum_m", bufs=2))
        psum_e = ctx.enter_context(tc.psum_pool(name="psum_e", bufs=2))
        psum_o = ctx.enter_context(tc.psum_pool(name="psum_o", bufs=1))

        st = {}

        def live(q):
            return 0 <= q < NPAIR

        def load(n):
            g_sb = gin.tile([P, LOADS[n], OUT], BF16, name="g_sb")
            nc.sync.dma_start(out=g_sb[:], in_=g_v[:, load_start[n] : load_start[n] + LOADS[n], :])
            st["g", n] = g_sb

        w_raw = keep.tile([P, 4, K], BF16)
        for u in range(2):
            nc.sync.dma_start(
                out=w_raw[:, 2 * u : 2 * u + 2, :],
                in_=w2[256 * u : 256 * u + 256, :].rearrange("(q e) c -> q e c", e=2),
            )
        xc = keep.tile([P, NT, IN], BF16)
        nc.sync.dma_start(out=xc[:, 0:X_HEAD, :], in_=x_v[:, 0:X_HEAD, :])
        load(0)
        load(1)
        nc.sync.dma_start(out=xc[:, X_HEAD:NT, :], in_=x_v[:, X_HEAD:NT, :])
        for n in range(2, G_BUFS):
            load(n)

        ident = keep.tile([P, P], F32)
        make_identity(nc, ident[:])
        ident_b = keep.tile([P, P], BF16)
        make_identity(nc, ident_b[:])

        nc.vector.tensor_scalar(
            out=xc[:, 0:X_HEAD, :], in0=xc[:, 0:X_HEAD, :], scalar1=-4.0, scalar2=4.0, op0=ALU.max, op1=ALU.min
        )
        w_grp = keep.tile([P, K, 4], BF16, align_bytes=64)
        w_view = w_raw[:].rearrange("p t (i g) -> p g i t", g=NB)
        for g in range(NB):
            eng = nc.vector if g < NB // 2 else nc.gpsimd
            eng.tensor_scalar(
                out=w_grp[:, g * IN : (g + 1) * IN, :],
                in0=w_view[:, g, :, :],
                scalar1=-1.0 if g in NEGATED else 1.0,
                scalar2=0.0,
                op0=ALU.mult,
                op1=ALU.add,
            )
        w_codes = keep.tile([P, K], U32, align_bytes=64)
        w_scales = keep.tile([P, K], U8, align_bytes=64)
        nc.vector.quantize_mx(
            out=w_codes[:].bitcast(E4X4),
            scales=w_scales[:],
            in_=w_grp[:].rearrange("p c t -> p (c t)"),
        )

        def x_transposes(b):
            xt = psum_x.tile([P, BLOCK, P], BF16, name="xt")
            for q in range(BLOCK):
                t = 2 * (BLOCK * b + q)
                nc.tensor.transpose(xt[:, q, :], xc[:, t : t + 2, :].rearrange("p t i -> p (t i)"), ident_b[:])
            st["xt", b] = xt

        def chain_a(n):
            w = GROUPS[n] * P
            b, off = divmod(group_start[n], BLOCK)
            xt = st["xt", b][:, off : off + GROUPS[n], :].rearrange("p q t -> p (q t)")
            a = two.tile([P, 2, w], F32, name="a")
            for k in range(2):
                nc.scalar.activation(out=a[:, k, :], in_=xt, func=ACT.Abs, bias=0.5 - k, scale=2.5)
            nc.scalar.activation(out=a[:], in_=a[:], func=ACT.Abs, bias=-2.0, scale=1.0)
            st["a", n] = a

        def chain_b(n):
            w = GROUPS[n] * P
            bh = two.tile([P, 2, w], F32, name="bh")
            nc.scalar.activation(out=bh[:], in_=st["a", n][:], func=ACT.Abs, bias=-1.0, scale=0.5)
            hq = two.tile([P, 2, w], F32, name="hq")
            nc.scalar.activation(out=hq[:], in_=bh[:], func=ACT.Abs, bias=-0.25, scale=0.5)
            nz = two.tile([P, 2, w], F32, name="nz")
            nc.gpsimd.tensor_scalar(out=nz[:], in0=bh[:], scalar1=-2.0, scalar2=1.0, op0=ALU.mult, op1=ALU.add)
            r = two.tile([P, 2, w], F32, name="r")
            for k in range(2):
                nc.gpsimd.tensor_tensor(out=r[:, k, :], in0=bh[:, 1 - k, :], in1=hq[:, k, :], op=ALU.subtract)
            cf = two.tile([P, GROUPS[n], 3, P], F32, name="cf")
            nc.gpsimd.tensor_tensor(
                out=cf[:, :, 0:2, :].rearrange("p q e t -> p e q t"),
                in0=nz[:].rearrange("p e (q t) -> p e q t", t=P),
                in1=r[:].rearrange("p e (q t) -> p e q t", t=P),
                op=ALU.mult,
            )
            nc.gpsimd.tensor_tensor(
                out=cf[:, :, 2, :],
                in0=nz[:, 0, :].rearrange("p (q t) -> p q t", t=P),
                in1=nz[:, 1, :].rearrange("p (q t) -> p q t", t=P),
                op=ALU.mult,
            )
            st["cf", n] = cf

        def distances(n, planes):
            t0 = 2 * group_start[n]
            if ("ab", n) not in st:
                ab_new = two.tile([P, NB, 2 * GROUPS[n], IN], F32, name="ab")
                st["ab", n] = ab_new
            for g in planes:
                nc.scalar.activation(
                    out=st["ab", n][:, g, :, :],
                    in_=xc[:, t0 : t0 + 2 * GROUPS[n], :],
                    func=ACT.Abs,
                    bias=3.5 - g,
                    scale=2.5,
                )

        def x_work(n, part):
            if part == 0:
                chain_a(n)
            elif part == 1:
                chain_b(n)
            elif part == 2:
                distances(n, range(0, NB // 2))
            else:
                distances(n, range(NB // 2, NB))

        def g_transposes(q):
            n, off = load_of[2 * q]
            g32 = st["g", n][:].bitcast(F32)
            pt = psum_t.tile([P, 2, 2, P], F32, name="pt")
            for j in range(2):
                for u in range(2):
                    nc.tensor.transpose(pt[:, j, u, :], g32[:, off + j, P * u : P * u + P], ident[:])
            st["pt", q] = pt
            if off + 2 == LOADS[n] and n + G_BUFS < len(LOADS):
                load(n + G_BUFS)

        def regroup(q):
            grp = three.tile([P, 2 * P, 2], F32, name="grp", align_bytes=64)
            nc.vector.tensor_copy(
                out=grp[:].rearrange("p (j r) u -> p j r u", j=2),
                in_=st["pt", q][:].rearrange("p j u r -> p j r u"),
            )
            st["grp", q] = grp

        def quantise(q):
            g_codes = three.tile([P, 2 * P], U32, name="g_codes", align_bytes=64)
            g_scales = three.tile([P, 2 * P], U8, name="g_scales", align_bytes=64)
            nc.vector.quantize_mx(
                out=g_codes[:].bitcast(E5X4),
                scales=g_scales[:],
                in_=st["grp", q][:].rearrange("p r u -> p (r u)").bitcast(BF16),
            )
            st["codes", q] = (g_codes, g_scales)

        def mx(q):
            g_codes, g_scales = st["codes", q]
            for j in range(2):
                pm = psum_m.tile([P, K], F32, name="pm")
                nc.tensor.matmul_mx(
                    out=pm[:],
                    lhsT=g_codes[:, j * P : (j + 1) * P].bitcast(E5X4),
                    lhsT_scale=g_scales[:, j * P : (j + 1) * P],
                    rhs=w_codes[:].bitcast(E4X4),
                    rhs_scale=w_scales[:],
                    start=True,
                    stop=True,
                )
                st["pm", q, j] = pm

        def products(q):
            n, off = group_of[q]
            if off == 0:
                tm_new = two.tile([P, NB, 2 * GROUPS[n], IN], F32, name="tm")
                st["tm", n] = tm_new
            for j in range(2):
                nc.vector.scalar_tensor_tensor(
                    out=st["tm", n][:, :, 2 * off + j, :],
                    in0=st["ab", n][:, :, 2 * off + j, :],
                    scalar=2.0,
                    in1=st["pm", q, j][:].rearrange("p (g i) -> p g i", g=NB),
                    op0=ALU.is_lt,
                    op1=ALU.mult,
                )

        def e_sums(q):
            n, off = group_of[q]
            eo = psum_e.tile([P, 3, P], F32, name="eo")
            for e, planes in enumerate(DIFFS):
                for m, g in enumerate(planes):
                    nc.tensor.matmul(
                        out=eo[:, e, :],
                        lhsT=st["tm", n][:, g, 2 * off : 2 * off + 2, :].rearrange("p t i -> p (t i)"),
                        rhs=ident[:],
                        start=(m == 0),
                        stop=(m == len(planes) - 1),
                        is_transpose=True,
                    )
            st["eo", q] = eo

        def weigh(q):
            n, off = group_of[q]
            pr = three.tile([P, 3, P], F32, name="pr")
            nc.vector.tensor_tensor(out=pr[:], in0=st["eo", q][:], in1=st["cf", n][:, off, :, :], op=ALU.mult)
            st["pr", q] = pr

        def o_sums(q):
            n, off = group_of[q]
            if off == 0:
                ob_new = psum_o.tile([P, GROUPS[n], P], F32, name="ob")
                st["ob", n] = ob_new
            for e in range(3):
                nc.tensor.matmul(
                    out=st["ob", n][:, off, :],
                    lhsT=st["pr", q][:, e, :],
                    rhs=ident[:],
                    start=(e == 0),
                    stop=(e == 2),
                    is_transpose=True,
                )

        def copy_out(n):
            o = two.tile([P, GROUPS[n] * P], F32, name="o")
            nc.scalar.activation(out=o[:], in_=st["ob", n][:].rearrange("p q t -> p (q t)"), func=ACT.Copy, scale=5.0)
            t0 = 2 * group_start[n]
            nc.sync.dma_start(out=o_v[:, t0 : t0 + 2 * GROUPS[n], :], in_=o[:].rearrange("p (t i) -> p t i", i=IN))

        x_transposes(0)
        for part in range(4):
            x_work(0, part)
        for q in range(-4, NPAIR + 3):
            if live(q - 3) and group_of[q - 3][1] == GROUPS[group_of[q - 3][0]] - 1:
                copy_out(group_of[q - 3][0])
            if live(q - 1):
                e_sums(q - 1)
            if live(q):
                products(q)
            if live(q - 2):
                o_sums(q - 2)
            if live(q + 4):
                g_transposes(q + 4)
            if live(q):
                n, off = group_of[q]
                nxt = n + 2
                if off == GROUPS[n] - 1 and nxt < len(GROUPS) and group_start[nxt] % BLOCK == 0:
                    x_transposes(group_start[nxt] // BLOCK)
            if live(q + 1):
                mx(q + 1)
            if live(q + 3):
                regroup(q + 3)
            if live(q + 2):
                quantise(q + 2)
            if live(q - 1):
                weigh(q - 1)
            if q == -1:
                nc.vector.tensor_scalar(
                    out=xc[:, X_HEAD:NT, :], in0=xc[:, X_HEAD:NT, :], scalar1=-4.0, scalar2=4.0, op0=ALU.max, op1=ALU.min
                )
            if live(q):
                n, off = group_of[q]
                if n + 1 < len(GROUPS):
                    for part in range(4 * off // GROUPS[n], 4 * (off + 1) // GROUPS[n]):
                        x_work(n + 1, part)
